import numpy as np
import ml_dtypes


def mxq(x, axis, fmt="e4m3"):
    dtype, down = {"e4m3": (ml_dtypes.float8_e4m3fn, 7), "e5m2": (ml_dtypes.float8_e5m2, 14)}[fmt]
    v = np.moveaxis(np.asarray(x, np.float32).astype(ml_dtypes.bfloat16).astype(np.float64), axis, -1)
    blocks = v.reshape(v.shape[:-1] + (-1, 32))
    amax = np.abs(blocks).max(-1, keepdims=True)
    byte = np.maximum(np.where(amax > 0, np.frexp(amax)[1] - 1 + 127, 0) - down, 1)
    scale = np.exp2(byte - 127.0)
    codes = (blocks / scale).astype(np.float32).astype(dtype).astype(np.float64)
    return np.moveaxis((codes * scale).reshape(v.shape), -1, axis)


WIDE = False


def mx_kscale(k):
    if not WIDE:
        return np.ones(k)
    levels = np.array([10, -10, 5, -5, 0])
    if k % 512:
        return np.exp2(np.random.permutation(np.resize(levels, k // 32))).repeat(32)
    a = np.empty((k // 512, 16))
    for p in range(k // 512):
        a[p, :8] = np.random.permutation(np.resize(levels, 8))
        for g in range(8):
            far = levels[np.abs(levels - a[p, g]) >= 10]
            a[p, g + 8] = far[np.random.randint(len(far))]
    return np.exp2(a.ravel()).repeat(32)


BF16 = ml_dtypes.bfloat16


def bf(x):
    return np.asarray(x, np.float32).astype(BF16)


def f64(x):
    return np.asarray(x).astype(np.float64)


B, I, H, C, S = 1024, 512, 1024, 511, 3
EPSILON = 1e-6
CC = 1 + C
K = I + H


def setup_inputs():
    s = mx_kscale(K)
    t = mx_kscale(CC)
    t = t / t.min()
    return {
        "invariant_input": bf(np.random.standard_normal((B, I)) * s[:I]),
        "equivariant_input": bf(np.random.standard_normal((B, S)) * 0.125 * t[0]),
        "invariant_hidden": bf(np.random.standard_normal((B, H)) * s[I:]),
        "equivariant_hidden": bf(np.random.standard_normal((B, S, C)) * 0.125 * t[1:]),
        "W_left": bf(np.random.standard_normal((CC, H)) * 0.15 / np.sqrt(CC) * t[:, None]),
        "W_right": bf(np.random.standard_normal((CC, H)) * 0.15 / np.sqrt(CC) * t[:, None]),
        "W_ii": bf(np.random.standard_normal((K, H)) * 0.6 / np.sqrt(K) / s[:, None]),
        "b_ii": bf(np.random.standard_normal(H) * 0.3),
    }


def reference(invariant_input, equivariant_input, invariant_hidden, equivariant_hidden, W_left, W_right, W_ii, b_ii):
    eq_comb = np.concatenate([f64(equivariant_input)[..., None], f64(equivariant_hidden)], axis=-1)
    inv_comb = np.concatenate([f64(invariant_input), f64(invariant_hidden)], axis=-1)
    norm = np.sum(eq_comb * eq_comb, axis=-2, keepdims=True) + EPSILON
    xn = mxq(eq_comb / norm, 2, "e4m3")
    left = xn @ mxq(f64(W_left), 0, "e4m3")
    right = xn @ mxq(f64(W_right), 0, "e4m3")
    proj = np.sum(left * right, axis=-2)
    lin = mxq(inv_comb, 1, "e4m3") @ mxq(f64(W_ii), 0, "e4m3")
    return np.tanh(proj + lin + f64(b_ii))

@@ -1,0 +1,371 @@
+from contextlib import ExitStack
+
+import concourse.mybir as mybir
+from concourse.masks import make_identity
+
+F32 = mybir.dt.float32
+BF16 = mybir.dt.bfloat16
+U32 = mybir.dt.uint32
+U8 = mybir.dt.uint8
+FP8X4 = mybir.dt.float8_e4m3fn_x4
+ACT = mybir.ActivationFunctionType
+ALU = mybir.AluOpType
+
+FLOPS = 2 * (2 * 3072 * 512 * 1024 + 1024 * 1536 * 1024)
+EPS = 1e-6
+P = 128
+GROUPS = 4
+ROUNDS = 16
+W_R, W_L, W_I = 0, 1, 2
+
+
+def tile_ryeelman_pa_kernel(
+    tc,
+    invariant_input,
+    equivariant_input,
+    invariant_hidden,
+    equivariant_hidden,
+    W_left,
+    W_right,
+    W_ii,
+    b_ii,
+    out,
+):
+    nc = tc.nc
+    with ExitStack() as ctx:
+        keep = ctx.enter_context(tc.tile_pool(name="keep", bufs=1))
+        acts = ctx.enter_context(tc.tile_pool(name="acts", bufs=3))
+        work = ctx.enter_context(tc.tile_pool(name="work", bufs=2))
+        stage = ctx.enter_context(tc.tile_pool(name="stage", bufs=2))
+        block = ctx.enter_context(tc.tile_pool(name="block", bufs=3))
+        ahead = ctx.enter_context(tc.psum_pool(name="ahead", bufs=3))
+        ring = ctx.enter_context(tc.psum_pool(name="ring", bufs=5))
+
+        zero = keep.tile([P, 1], F32)
+        nc.vector.memset(zero[:], 0.0)
+        eps = keep.tile([P, 1], F32)
+        nc.vector.tensor_scalar_add(out=eps[:], in0=zero[:], scalar1=EPS)
+        warm = keep.tile([P, 1], F32)
+        nc.scalar.activation(out=warm[:], in_=eps[:], func=ACT.Abs_reciprocal_sqrt)
+        ident = keep.tile([P, P], F32)
+        make_identity(nc, ident[:])
+        ident_bf = keep.tile([P, P], BF16)
+        make_identity(nc, ident_bf[:])
+
+        head_hidden = keep.tile([P, 24, 16], BF16)
+        head_input = keep.tile([P, 24], BF16)
+        bias_rows = keep.tile([P, P], BF16)
+        bias = keep.tile([P, 8], F32)
+        w_codes = keep.tile([P, 5, 1024], U32, align_bytes=64)
+        w_scales = keep.tile([P, 5, 1024], U8, align_bytes=64)
+        x_codes = keep.tile([P, 3, 1024], U32, align_bytes=64)
+        x_scales = keep.tile([P, 3, 1024], U8, align_bytes=64)
+        i_codes = keep.tile([P, 3, 1024], U32, align_bytes=64)
+        i_scales = keep.tile([P, 3, 1024], U8, align_bytes=64)
+
+        hidden_rows = equivariant_hidden.rearrange("(p s) j c -> p (s j) c", s=8)
+        input_rows = invariant_input.rearrange("(p s) c -> p s c", s=8)
+        state_rows = invariant_hidden.rearrange("(p s) c -> p s c", s=8)
+        out_rows = out.rearrange("(p s) h -> p s h", s=8)
+        w_hbm = (W_right, W_left, W_ii[0:512, :], W_ii[512:1024, :], W_ii[1024:1536, :])
+
+        eq_sb, inv_sb, w_raw, w_grouped = {}, {}, {}, {}
+        banks, squares, recip, x_grouped, i_grouped, terms, turned = {}, {}, {}, {}, {}, {}, {}
+
+        def load_eq(g):
+            eq = acts.tile([P, 6, 512], BF16, tag="eq", bufs=GROUPS, align_bytes=64)
+            nc.sync.dma_start(out=eq[:, :, 16:512], in_=hidden_rows[:, 6 * g : 6 * g + 6, 15:511])
+            eq_sb[g] = eq
+
+        def heads(g):
+            nc.vector.tensor_copy(out=eq_sb[g][:, :, 1:16], in_=head_hidden[:, 6 * g : 6 * g + 6, 0:15])
+            nc.vector.tensor_copy(out=eq_sb[g][:, :, 0:1], in_=head_input[:, 6 * g : 6 * g + 6].unsqueeze(2))
+
+        def load_inv(g):
+            iv = acts.tile([P, 2, 1536], BF16, tag="inv", align_bytes=64)
+            nc.sync.dma_start(out=iv[:, :, 0:512], in_=input_rows[:, 2 * g : 2 * g + 2, :])
+            nc.sync.dma_start(out=iv[:, :, 512:1536], in_=state_rows[:, 2 * g : 2 * g + 2, :])
+            inv_sb[g] = iv
+
+        def load_w(w, half):
+            raw = stage.tile([P, 4, 512], BF16, tag="raw", bufs=5)
+            nc.sync.dma_start(
+                out=raw[:], in_=w_hbm[w][:, 512 * half : 512 * half + 512].rearrange("(p t) c -> p t c", t=4)
+            )
+            w_raw[(w, half)] = raw
+
+        def regroup_w(w, half):
+            grouped = stage.tile([P, 512, 4], BF16, tag="grouped", align_bytes=64)
+            nc.vector.tensor_copy(
+                out=grouped[:].rearrange("p (c i) t -> p c t i", i=4),
+                in_=w_raw[(w, half)][:].rearrange("p t (c i) -> p c t i", i=4),
+            )
+            w_grouped[(w, half)] = grouped
+
+        def quantise_w(w, half):
+            cols = slice(512 * half, 512 * half + 512)
+            nc.vector.quantize_mx(
+                out=w_codes[:, w, cols].bitcast(FP8X4),
+                scales=w_scales[:, w, cols],
+                in_=w_grouped[(w, half)][:].rearrange("p c t -> p (c t)"),
+            )
+
+        def by_word(ap):
+            return ap.rearrange("p (b u e) -> p b u e", u=2, e=2)
+
+        def eq_bank(g, j, pool=ahead, tag="ahead"):
+            words = eq_sb[g][:].bitcast(F32)
+            bank = pool.tile([P, 2, 2, P], F32, tag=tag)
+            for u in range(2):
+                for s in range(2):
+                    nc.tensor.transpose(bank[:, u, s, :], words[:, 3 * s + j, u::2], ident[:])
+            banks[("eq", g, j)] = bank[:].bitcast(BF16).rearrange("p u s (b e) -> p (s b) u e", e=2)
+
+        def square(g, j):
+            sq = work.tile([P, 1024], F32, tag="square%d" % j)
+            nc.scalar.activation(out=by_word(sq[:]), in_=banks[("eq", g, j)], func=ACT.Square)
+            squares[(g, j)] = sq
+
+        def add_square(engine, g, j):
+            engine.tensor_tensor(out=squares[(g, 0)][:], in0=squares[(g, 0)][:], in1=squares[(g, j)][:], op=ALU.add)
+
+        def reciprocal(g):
+            nc.scalar.activation(
+                out=squares[(g, 1)][:], in_=squares[(g, 0)][:], func=ACT.Abs_reciprocal_sqrt, bias=eps[:]
+            )
+            r = work.tile([P, 1024], F32, tag="recip", bufs=3)
+            nc.scalar.activation(out=r[:], in_=squares[(g, 1)][:], func=ACT.Square)
+            recip[g] = r
+
+        def scale_eq(g, j):
+            xg = work.tile([P, 1024], BF16, tag="x_grouped", bufs=3, align_bytes=64)
+            nc.vector.tensor_tensor(
+                out=by_word(xg[:]), in0=banks[("eq", g, j)], in1=by_word(recip[g][:]), op=ALU.mult
+            )
+            x_grouped[(g, j)] = xg
+
+        def quantise_x(g, j):
+            cols = slice(256 * g, 256 * g + 256)
+            nc.vector.quantize_mx(
+                out=x_codes[:, j, cols].bitcast(FP8X4), scales=x_scales[:, j, cols], in_=x_grouped[(g, j)][:]
+            )
+
+        def inv_bank(g, k):
+            words = inv_sb[g][:].bitcast(F32)
+            bank = ahead.tile([P, 2, 2, P], F32, tag="ahead")
+            for u in range(2):
+                for s in range(2):
+                    nc.tensor.transpose(bank[:, u, s, :], words[:, s, 256 * k + u : 256 * k + 256 : 2], ident[:])
+            banks[("inv", g, k)] = bank[:].rearrange("p u s b -> p (s b) u")
+
+        def copy_inv(g, k):
+            ig = work.tile([P, 1024], BF16, tag="i_grouped", bufs=3, align_bytes=64)
+            nc.scalar.copy(out=ig[:].bitcast(F32).rearrange("p (b u) -> p b u", u=2), in_=banks[("inv", g, k)])
+            i_grouped[(g, k)] = ig
+
+        def quantise_inv(g, k):
+            cols = slice(256 * g, 256 * g + 256)
+            nc.vector.quantize_mx(
+                out=i_codes[:, k, cols].bitcast(FP8X4), scales=i_scales[:, k, cols], in_=i_grouped[(g, k)][:]
+            )
+
+        def mx(acc, w, h_tile, codes, scales, row, g, start, stop):
+            h_cols = slice(128 * h_tile, 128 * h_tile + 128)
+            b_cols = slice(256 * g, 256 * g + 256)
+            nc.tensor.matmul_mx(
+                out=acc,
+                lhsT=w_codes[:, w, h_cols].bitcast(FP8X4),
+                lhsT_scale=w_scales[:, w, h_cols],
+                rhs=codes[:, row, b_cols].bitcast(FP8X4),
+                rhs_scale=scales[:, row, b_cols],
+                start=start,
+                stop=stop,
+            )
+
+        def products(r):
+            g, quarter = r // 4, r % 4
+            copies = []
+            for j in range(3):
+                right = ring.tile([P, 2, 256], F32, tag="ring")
+                for i in range(2):
+                    mx(right[:, i, :], W_R, 2 * quarter + i, x_codes, x_scales, j, g, True, True)
+                right_sb = block.tile([P, 2, 256], F32, tag="right", bufs=4)
+                nc.scalar.copy(out=right_sb[:], in_=right[:])
+                copies.append(right_sb)
+            for j in range(3):
+                left = ring.tile([P, 2, 256], F32, tag="ring")
+                for i in range(2):
+                    mx(left[:, i, :], W_L, 2 * quarter + i, x_codes, x_scales, j, g, True, True)
+                term = block.tile([P, 2, 256], F32, tag="term%d" % j, bufs=6)
+                nc.vector.tensor_tensor(out=term[:], in0=left[:], in1=copies[j][:], op=ALU.mult)
+                terms[(r, j)] = term
+
+        def linear(r):
+            g, quarter = r // 4, r % 4
+            lin = ring.tile([P, 2, 256], F32, tag="ring")
+            for i in range(2):
+                for k in range(3):
+                    mx(lin[:, i, :], W_I + k, 2 * quarter + i, i_codes, i_scales, k, g, k == 0, k == 2)
+            for i in range(2):
+                nc.vector.scalar_tensor_tensor(
+                    out=terms[(r, 0)][:, i, :],
+                    in0=lin[:, i, :],
+                    scalar=bias[:, 2 * quarter + i : 2 * quarter + i + 1],
+                    in1=terms[(r, 0)][:, i, :],
+                    op0=ALU.add,
+                    op1=ALU.add,
+                )
+
+        def tensor_adds(r):
+            return r < 4 or r >= ROUNDS - 2
+
+        def add_terms(r, j):
+            if not tensor_adds(r):
+                nc.gpsimd.tensor_tensor(out=terms[(r, j - 1)][:], in0=terms[(r, j - 1)][:], in1=terms[(r, j)][:], op=ALU.add)
+
+        def turn_back(r):
+            bank = ring.tile([P, 2, 2, P], F32, tag="ring")
+            n_terms = 3 if tensor_adds(r) else 1
+            for s in range(2):
+                for i in range(2):
+                    for j in range(n_terms):
+                        nc.tensor.matmul(
+                            out=bank[:, s, i, :],
+                            lhsT=terms[(r, j)][:, i, 128 * s : 128 * s + 128],
+                            rhs=ident[:],
+                            is_transpose=True,
+                            start=(j == 0),
+                            stop=(j == n_terms - 1),
+                        )
+            turned[r] = bank
+
+        def finish(r):
+            g, quarter = r // 4, r % 4
+            res = block.tile([P, 2, 256], F32, tag="res")
+            nc.scalar.activation(out=res[:], in_=turned[r][:].rearrange("p s i h -> p s (i h)"), func=ACT.Tanh)
+            nc.sync.dma_start(out=out_rows[:, 2 * g : 2 * g + 2, 256 * quarter : 256 * quarter + 256], in_=res[:])
+
+        with nc.allow_non_contiguous_dma(reason="the first 16 channels arrive in short runs"):
+            nc.scalar.dma_start(out=head_input[:], in_=equivariant_input.rearrange("(p s) j -> p (s j)", s=8))
+            nc.scalar.dma_start(out=head_hidden[:, 0:6, 0:15], in_=hidden_rows[:, 0:6, 0:15])
+            nc.scalar.dma_start(out=head_hidden[:, 6:24, 0:15], in_=hidden_rows[:, 6:24, 0:15])
+        nc.vector.memset(bias_rows[:], 0.0)
+        nc.gpsimd.dma_start(out=bias_rows[0:8, :], in_=b_ii.rearrange("(r c) -> r c", c=P))
+        load_eq(0)
+        load_w(W_R, 0)
+        load_w(W_L, 0)
+        load_eq(1)
+        load_w(W_I, 0)
+        load_inv(0)
+        load_w(W_I + 1, 0)
+        load_w(W_I + 2, 0)
+        load_eq(2)
+        load_eq(3)
+        load_inv(1)
+
+        heads(0)
+        for j in range(3):
+            eq_bank(0, j)
+        for w in (W_R, W_L):
+            regroup_w(w, 0)
+        for j in range(3):
+            square(0, j)
+            if j:
+                add_square(nc.vector, 0, j)
+        reciprocal(0)
+        for w in (W_R, W_L):
+            quantise_w(w, 0)
+            load_w(w, 1)
+        heads(1)
+        bias_ps = ring.tile([P, P], BF16, tag="ring")
+        nc.tensor.transpose(bias_ps[:], bias_rows[:], ident_bf[:])
+        nc.vector.tensor_copy(out=bias[:], in_=bias_ps[:, 0:8])
+        heads(2)
+        heads(3)
+        for j in range(3):
+            eq_bank(0, j)
+        for j in range(3):
+            eq_bank(1, j, ring, "ring")
+        for j in range(3):
+            scale_eq(0, j)
+            quantise_x(0, j)
+            square(1, j)
+        for j in (1, 2):
+            add_square(nc.vector, 1, j)
+
+        def banks_for(r):
+            g, quarter = r // 4, r % 4
+            if quarter == 0 and g < GROUPS:
+                for k in range(3):
+                    inv_bank(g, k)
+            if r in (1, 2):
+                for j in range(3):
+                    eq_bank(r + 1, j)
+            if r == 3:
+                for j in range(3):
+                    eq_bank(1, j)
+            if 1 <= g < GROUPS - 1 and quarter:
+                eq_bank(g + 1, quarter - 1)
+
+        def before_products(r):
+            g, quarter = r // 4, r % 4
+            if 1 <= g < GROUPS - 1 and quarter:
+                scale_eq(g + 1, quarter - 1)
+                quantise_x(g + 1, quarter - 1)
+
+        def side_work(r):
+            g, quarter = r // 4, r % 4
+            if quarter == 0 and g < GROUPS:
+                for k in range(3):
+                    copy_inv(g, k)
+            if r == 0:
+                for k in range(3):
+                    regroup_w(W_I + k, 0)
+                    quantise_w(W_I + k, 0)
+                    load_w(W_I + k, 1)
+                load_inv(2)
+                load_inv(3)
+                reciprocal(1)
+            if r == 1:
+                for w in (W_R, W_L):
+                    regroup_w(w, 1)
+                    quantise_w(w, 1)
+            if r == 2:
+                for k in range(3):
+                    regroup_w(W_I + k, 1)
+                    quantise_w(W_I + k, 1)
+            if quarter == 0 and g < GROUPS:
+                for k in range(3):
+                    quantise_inv(g, k)
+            if r in (1, 2):
+                for j in range(3):
+                    square(r + 1, j)
+                    if j:
+                        add_square(nc.gpsimd, r + 1, j)
+            if r in (2, 3):
+                reciprocal(r)
+            if r == 3:
+                for j in range(3):
+                    scale_eq(1, j)
+                    quantise_x(1, j)
+
+        for r in range(ROUNDS + 2):
+            before_products(r)
+            if r < ROUNDS:
+                products(r)
+                add_terms(r, 2)
+            if r == 0:
+                banks_for(0)
+            if 1 <= r <= ROUNDS:
+                linear(r - 1)
+                add_terms(r - 1, 1)
+            side_work(r)
+            due = [v for v in range(ROUNDS) if max(v + 2, 3 + v // 2) == r]
+            for v in due[:-1]:
+                turn_back(v)
+                finish(v)
+            for v in due[-1:]:
+                turn_back(v)
+            banks_for(r + 1)
+            for v in due[-1:]:
+                finish(v)

@@ -15,7 +15,8 @@ FLOPS = 2 * (2 * 3072 * 512 * 1024 + 1024 * 1536 * 1024)
 EPS = 1e-6
 P = 128
 GROUPS = 4
-ROUNDS = 16
+ORDER = [(g, q) for half in ((0, 1), (2, 3)) for g in (0, 1) for q in half] + [(g, q) for g in (2, 3) for q in range(4)]
+ROUNDS = len(ORDER)
 W_R, W_L, W_I = 0, 1, 2
 
 
@@ -113,34 +114,68 @@ def tile_ryeelman_pa_kernel(
         def by_word(ap):
             return ap.rearrange("p (b u e) -> p b u e", u=2, e=2)
 
-        def eq_bank(g, j, pool=ahead, tag="ahead"):
+        def square(engine, g, s):
+            if g not in squares:
+                sq_tile = work.tile([P, 6, 4, P], F32, tag="square")
+                squares[g] = sq_tile
+            rows = slice(3 * s, 3 * s + 3)
+            src = eq_sb[g][:, rows, :].rearrange("p r (k t) -> p r t k", t=4)
+            dst = squares[g][:, rows, :, :]
+            if engine is nc.scalar:
+                nc.scalar.activation(out=dst, in_=src, func=ACT.Square)
+            else:
+                nc.vector.tensor_tensor(out=dst, in0=src, in1=src, op=ALU.mult)
+
+        def norm_bank(g, s):
+            bank = ahead.tile([P, 4, P], F32, tag="ahead")
+            for t in range(4):
+                for j in range(3):
+                    nc.tensor.matmul(
+                        out=bank[:, t, :],
+                        lhsT=squares[g][:, 3 * s + j, t, :],
+                        rhs=ident[:],
+                        is_transpose=True,
+                        start=(j == 0),
+                        stop=(j == 2),
+                    )
+            banks[("norm", g, s)] = bank[:].rearrange("p t b -> p b t")
+
+        def reciprocal(g, s):
+            if g not in recip:
+                r_tile = work.tile([P, 2, 512], F32, tag="recip", bufs=3)
+                recip[g] = r_tile
+            root = work.tile([P, 512], F32, tag="root")
+            nc.scalar.activation(
+                out=root[:].rearrange("p (b t) -> p b t", t=4),
+                in_=banks[("norm", g, s)],
+                func=ACT.Abs_reciprocal_sqrt,
+                bias=eps[:],
+            )
+            nc.scalar.activation(out=recip[g][:, s, :], in_=root[:], func=ACT.Square)
+
+        def norm(g):
+            for s in range(2):
+                square(nc.scalar, g, s)
+            for s in range(2):
+                norm_bank(g, s)
+            for s in range(2):
+                reciprocal(g, s)
+
+        def eq_bank(g, j):
             words = eq_sb[g][:].bitcast(F32)
-            bank = pool.tile([P, 2, 2, P], F32, tag=tag)
+            bank = ahead.tile([P, 2, 2, P], F32, tag="ahead")
             for u in range(2):
                 for s in range(2):
                     nc.tensor.transpose(bank[:, u, s, :], words[:, 3 * s + j, u::2], ident[:])
             banks[("eq", g, j)] = bank[:].bitcast(BF16).rearrange("p u s (b e) -> p (s b) u e", e=2)
 
-        def square(g, j):
-            sq = work.tile([P, 1024], F32, tag="square%d" % j)
-            nc.scalar.activation(out=by_word(sq[:]), in_=banks[("eq", g, j)], func=ACT.Square)
-            squares[(g, j)] = sq
-
-        def add_square(engine, g, j):
-            engine.tensor_tensor(out=squares[(g, 0)][:], in0=squares[(g, 0)][:], in1=squares[(g, j)][:], op=ALU.add)
-
-        def reciprocal(g):
-            nc.scalar.activation(
-                out=squares[(g, 1)][:], in_=squares[(g, 0)][:], func=ACT.Abs_reciprocal_sqrt, bias=eps[:]
-            )
-            r = work.tile([P, 1024], F32, tag="recip", bufs=3)
-            nc.scalar.activation(out=r[:], in_=squares[(g, 1)][:], func=ACT.Square)
-            recip[g] = r
-
         def scale_eq(g, j):
             xg = work.tile([P, 1024], BF16, tag="x_grouped", bufs=3, align_bytes=64)
             nc.vector.tensor_tensor(
-                out=by_word(xg[:]), in0=banks[("eq", g, j)], in1=by_word(recip[g][:]), op=ALU.mult
+                out=by_word(xg[:]),
+                in0=banks[("eq", g, j)],
+                in1=by_word(recip[g][:].rearrange("p s c -> p (s c)")),
+                op=ALU.mult,
             )
             x_grouped[(g, j)] = xg
 
@@ -183,7 +218,7 @@ def tile_ryeelman_pa_kernel(
             )
 
         def products(r):
-            g, quarter = r // 4, r % 4
+            g, quarter = ORDER[r]
             copies = []
             for j in range(3):
                 right = ring.tile([P, 2, 256], F32, tag="ring")
@@ -201,7 +236,7 @@ def tile_ryeelman_pa_kernel(
                 terms[(r, j)] = term
 
         def linear(r):
-            g, quarter = r // 4, r % 4
+            g, quarter = ORDER[r]
             lin = ring.tile([P, 2, 256], F32, tag="ring")
             for i in range(2):
                 for k in range(3):
@@ -217,7 +252,7 @@ def tile_ryeelman_pa_kernel(
                 )
 
         def tensor_adds(r):
-            return r < 4 or r >= ROUNDS - 2
+            return r < 8 or r >= ROUNDS - 2
 
         def add_terms(r, j):
             if not tensor_adds(r):
@@ -240,84 +275,75 @@ def tile_ryeelman_pa_kernel(
             turned[r] = bank
 
         def finish(r):
-            g, quarter = r // 4, r % 4
+            g, quarter = ORDER[r]
             res = block.tile([P, 2, 256], F32, tag="res")
             nc.scalar.activation(out=res[:], in_=turned[r][:].rearrange("p s i h -> p s (i h)"), func=ACT.Tanh)
             nc.sync.dma_start(out=out_rows[:, 2 * g : 2 * g + 2, 256 * quarter : 256 * quarter + 256], in_=res[:])
 
         with nc.allow_non_contiguous_dma(reason="the first 16 channels arrive in short runs"):
-            nc.scalar.dma_start(out=head_input[:], in_=equivariant_input.rearrange("(p s) j -> p (s j)", s=8))
-            nc.scalar.dma_start(out=head_hidden[:, 0:6, 0:15], in_=hidden_rows[:, 0:6, 0:15])
+            nc.sync.dma_start(out=head_hidden[:, 0:6, 0:15], in_=hidden_rows[:, 0:6, 0:15])
+            nc.sync.dma_start(out=head_input[:], in_=equivariant_input.rearrange("(p s) j -> p (s j)", s=8))
+            load_eq(0)
             nc.scalar.dma_start(out=head_hidden[:, 6:24, 0:15], in_=hidden_rows[:, 6:24, 0:15])
         nc.vector.memset(bias_rows[:], 0.0)
         nc.gpsimd.dma_start(out=bias_rows[0:8, :], in_=b_ii.rearrange("(r c) -> r c", c=P))
-        load_eq(0)
         load_w(W_R, 0)
         load_w(W_L, 0)
         load_eq(1)
-        load_w(W_I, 0)
+        for k in range(3):
+            load_w(W_I + k, 0)
         load_inv(0)
-        load_w(W_I + 1, 0)
-        load_w(W_I + 2, 0)
         load_eq(2)
         load_eq(3)
         load_inv(1)
 
         heads(0)
-        for j in range(3):
-            eq_bank(0, j)
+        square(nc.scalar, 0, 0)
+        square(nc.vector, 0, 1)
+        for s in range(2):
+            norm_bank(0, s)
+            reciprocal(0, s)
         for w in (W_R, W_L):
             regroup_w(w, 0)
-        for j in range(3):
-            square(0, j)
-            if j:
-                add_square(nc.vector, 0, j)
-        reciprocal(0)
+        heads(1)
         for w in (W_R, W_L):
             quantise_w(w, 0)
             load_w(w, 1)
-        heads(1)
+        for j in range(3):
+            eq_bank(0, j)
+        for j in range(3):
+            scale_eq(0, j)
+            quantise_x(0, j)
+        norm(1)
         bias_ps = ring.tile([P, P], BF16, tag="ring")
         nc.tensor.transpose(bias_ps[:], bias_rows[:], ident_bf[:])
         nc.vector.tensor_copy(out=bias[:], in_=bias_ps[:, 0:8])
         heads(2)
         heads(3)
-        for j in range(3):
-            eq_bank(0, j)
-        for j in range(3):
-            eq_bank(1, j, ring, "ring")
-        for j in range(3):
-            scale_eq(0, j)
-            quantise_x(0, j)
-            square(1, j)
-        for j in (1, 2):
-            add_square(nc.vector, 1, j)
+
+        INV_ROUND = {0: 0, 2: 1, 8: 2, 12: 3}
+        X_ROUND = {1: [(1, 0), (1, 1), (1, 2)]}
+        for g in (2, 3):
+            for j in range(3):
+                X_ROUND[4 * g - 3 + j] = [(g, j)]
 
         def banks_for(r):
-            g, quarter = r // 4, r % 4
-            if quarter == 0 and g < GROUPS:
+            if r in INV_ROUND:
                 for k in range(3):
-                    inv_bank(g, k)
-            if r in (1, 2):
-                for j in range(3):
-                    eq_bank(r + 1, j)
-            if r == 3:
-                for j in range(3):
-                    eq_bank(1, j)
-            if 1 <= g < GROUPS - 1 and quarter:
-                eq_bank(g + 1, quarter - 1)
+                    inv_bank(INV_ROUND[r], k)
+            for g, j in X_ROUND.get(r, []):
+                eq_bank(g, j)
 
         def before_products(r):
-            g, quarter = r // 4, r % 4
-            if 1 <= g < GROUPS - 1 and quarter:
-                scale_eq(g + 1, quarter - 1)
-                quantise_x(g + 1, quarter - 1)
+            for g, j in X_ROUND.get(r, []):
+                if g > 1:
+                    scale_eq(g, j)
+                    quantise_x(g, j)
 
         def side_work(r):
-            g, quarter = r // 4, r % 4
-            if quarter == 0 and g < GROUPS:
+            if r in INV_ROUND:
                 for k in range(3):
-                    copy_inv(g, k)
+                    copy_inv(INV_ROUND[r], k)
             if r == 0:
                 for k in range(3):
                     regroup_w(W_I + k, 0)
@@ -325,29 +351,23 @@ def tile_ryeelman_pa_kernel(
                     load_w(W_I + k, 1)
                 load_inv(2)
                 load_inv(3)
-                reciprocal(1)
+                norm(2)
             if r == 1:
-                for w in (W_R, W_L):
-                    regroup_w(w, 1)
-                    quantise_w(w, 1)
-            if r == 2:
-                for k in range(3):
-                    regroup_w(W_I + k, 1)
-                    quantise_w(W_I + k, 1)
-            if quarter == 0 and g < GROUPS:
-                for k in range(3):
-                    quantise_inv(g, k)
-            if r in (1, 2):
-                for j in range(3):
-                    square(r + 1, j)
-                    if j:
-                        add_square(nc.gpsimd, r + 1, j)
-            if r in (2, 3):
-                reciprocal(r)
-            if r == 3:
                 for j in range(3):
                     scale_eq(1, j)
                     quantise_x(1, j)
+                norm(3)
+            if r == 2:
+                for w in (W_R, W_L):
+                    regroup_w(w, 1)
+                    quantise_w(w, 1)
+            if r == 3:
+                for k in range(3):
+                    regroup_w(W_I + k, 1)
+                    quantise_w(W_I + k, 1)
+            if r in INV_ROUND:
+                for k in range(3):
+                    quantise_inv(INV_ROUND[r], k)
 
         for r in range(ROUNDS + 2):
             before_products(r)
@@ -360,7 +380,7 @@ def tile_ryeelman_pa_kernel(
                 linear(r - 1)
                 add_terms(r - 1, 1)
             side_work(r)
-            due = [v for v in range(ROUNDS) if max(v + 2, 3 + v // 2) == r]
+            due = [v for v in range(ROUNDS) if v + 2 == r]
             for v in due[:-1]:
                 turn_back(v)
                 finish(v)

@@ -71,35 +71,36 @@ def tile_ryeelman_pa_kernel(
         w_hbm = (W_right, W_left, W_ii[0:512, :], W_ii[512:1024, :], W_ii[1024:1536, :])
 
         eq_sb, inv_sb, w_raw, w_grouped = {}, {}, {}, {}
-        banks, squares, recip, x_grouped, i_grouped, terms, turned = {}, {}, {}, {}, {}, {}, {}
+        banks, squares, recip, x_grouped, i_grouped, terms, turned, rights = {}, {}, {}, {}, {}, {}, {}, {}
 
-        def load_eq(g):
-            eq = acts.tile([P, 6, 512], BF16, tag="eq", bufs=GROUPS, align_bytes=64)
-            nc.sync.dma_start(out=eq[:, :, 16:512], in_=hidden_rows[:, 6 * g : 6 * g + 6, 15:511])
+        def load_eq(g, pieces=1):
+            eq = acts.tile([P, 6, 512], BF16, tag="eq", align_bytes=64)
+            n = 6 // pieces
+            for i in range(0, 6, n):
+                nc.sync.dma_start(out=eq[:, i : i + n, 16:512], in_=hidden_rows[:, 6 * g + i : 6 * g + i + n, 15:511])
             eq_sb[g] = eq
 
         def heads(g):
             nc.vector.tensor_copy(out=eq_sb[g][:, :, 1:16], in_=head_hidden[:, 6 * g : 6 * g + 6, 0:15])
             nc.vector.tensor_copy(out=eq_sb[g][:, :, 0:1], in_=head_input[:, 6 * g : 6 * g + 6].unsqueeze(2))
 
-        def load_inv(g):
-            iv = acts.tile([P, 2, 1536], BF16, tag="inv", align_bytes=64)
-            nc.sync.dma_start(out=iv[:, :, 0:512], in_=input_rows[:, 2 * g : 2 * g + 2, :])
-            nc.sync.dma_start(out=iv[:, :, 512:1536], in_=state_rows[:, 2 * g : 2 * g + 2, :])
-            inv_sb[g] = iv
+        def load_inv(pair):
+            first = acts.tile([P, 4, 512], BF16, tag="inv_input", bufs=2, align_bytes=64)
+            nc.sync.dma_start(out=first[:], in_=input_rows[:, 4 * pair : 4 * pair + 4, :])
+            rest = acts.tile([P, 4, 1024], BF16, tag="inv_state", bufs=2, align_bytes=64)
+            nc.sync.dma_start(out=rest[:], in_=state_rows[:, 4 * pair : 4 * pair + 4, :])
+            inv_sb[pair] = (first, rest)
 
-        def load_w(w, half):
-            raw = stage.tile([P, 4, 512], BF16, tag="raw", bufs=5)
-            nc.sync.dma_start(
-                out=raw[:], in_=w_hbm[w][:, 512 * half : 512 * half + 512].rearrange("(p t) c -> p t c", t=4)
-            )
-            w_raw[(w, half)] = raw
+        def load_w(w):
+            raw = stage.tile([P, 4, 1024], BF16, tag="raw", bufs=5)
+            nc.sync.dma_start(out=raw[:], in_=w_hbm[w].rearrange("(p t) c -> p t c", t=4))
+            w_raw[w] = raw
 
         def regroup_w(w, half):
             grouped = stage.tile([P, 512, 4], BF16, tag="grouped", align_bytes=64)
             nc.vector.tensor_copy(
                 out=grouped[:].rearrange("p (c i) t -> p c t i", i=4),
-                in_=w_raw[(w, half)][:].rearrange("p t (c i) -> p c t i", i=4),
+                in_=w_raw[w][:, :, 512 * half : 512 * half + 512].rearrange("p t (c i) -> p c t i", i=4),
             )
             w_grouped[(w, half)] = grouped
 
@@ -114,25 +115,24 @@ def tile_ryeelman_pa_kernel(
         def by_word(ap):
             return ap.rearrange("p (b u e) -> p b u e", u=2, e=2)
 
-        def square(engine, g, s):
-            if g not in squares:
-                sq_tile = work.tile([P, 6, 4, P], F32, tag="square")
-                squares[g] = sq_tile
-            rows = slice(3 * s, 3 * s + 3)
-            src = eq_sb[g][:, rows, :].rearrange("p r (k t) -> p r t k", t=4)
-            dst = squares[g][:, rows, :, :]
-            if engine is nc.scalar:
-                nc.scalar.activation(out=dst, in_=src, func=ACT.Square)
-            else:
-                nc.vector.tensor_tensor(out=dst, in0=src, in1=src, op=ALU.mult)
+        def square(engine, g, s, rows=((0, 3),)):
+            sq_tile = work.tile([P, 3, 4, P], F32, tag="square")
+            squares[(g, s)] = sq_tile
+            for lo, hi in rows:
+                src = eq_sb[g][:, 3 * s + lo : 3 * s + hi, :].rearrange("p r (k t) -> p r t k", t=4)
+                dst = sq_tile[:, lo:hi, :, :]
+                if engine is nc.scalar:
+                    nc.scalar.activation(out=dst, in_=src, func=ACT.Square)
+                else:
+                    nc.vector.tensor_tensor(out=dst, in0=src, in1=src, op=ALU.mult)
 
-        def norm_bank(g, s):
-            bank = ahead.tile([P, 4, P], F32, tag="ahead")
+        def norm_bank(g, s, pool=ahead, tag="ahead"):
+            bank = pool.tile([P, 4, P], F32, tag=tag)
             for t in range(4):
                 for j in range(3):
                     nc.tensor.matmul(
                         out=bank[:, t, :],
-                        lhsT=squares[g][:, 3 * s + j, t, :],
+                        lhsT=squares[(g, s)][:, j, t, :],
                         rhs=ident[:],
                         is_transpose=True,
                         start=(j == 0),
@@ -142,7 +142,7 @@ def tile_ryeelman_pa_kernel(
 
         def reciprocal(g, s):
             if g not in recip:
-                r_tile = work.tile([P, 2, 512], F32, tag="recip", bufs=3)
+                r_tile = work.tile([P, 2, 512], F32, tag="recip")
                 recip[g] = r_tile
             root = work.tile([P, 512], F32, tag="root")
             nc.scalar.activation(
@@ -153,9 +153,11 @@ def tile_ryeelman_pa_kernel(
             )
             nc.scalar.activation(out=recip[g][:, s, :], in_=root[:], func=ACT.Square)
 
-        def norm(g):
+        def squares_of(g):
             for s in range(2):
-                square(nc.scalar, g, s)
+                square(nc.scalar, g, s, rows=((0, 1), (1, 2), (2, 3)))
+
+        def norm(g):
             for s in range(2):
                 norm_bank(g, s)
             for s in range(2):
@@ -169,15 +171,17 @@ def tile_ryeelman_pa_kernel(
                     nc.tensor.transpose(bank[:, u, s, :], words[:, 3 * s + j, u::2], ident[:])
             banks[("eq", g, j)] = bank[:].bitcast(BF16).rearrange("p u s (b e) -> p (s b) u e", e=2)
 
-        def scale_eq(g, j):
-            xg = work.tile([P, 1024], BF16, tag="x_grouped", bufs=3, align_bytes=64)
+        def scale_eq(g, j, slots=(0, 2)):
+            if (g, j) not in x_grouped:
+                xg = work.tile([P, 1024], BF16, tag="x_grouped", bufs=3, align_bytes=64)
+                x_grouped[(g, j)] = xg
+            lo, hi = slots
             nc.vector.tensor_tensor(
-                out=by_word(xg[:]),
-                in0=banks[("eq", g, j)],
-                in1=by_word(recip[g][:].rearrange("p s c -> p (s c)")),
+                out=by_word(x_grouped[(g, j)][:, 512 * lo : 512 * hi]),
+                in0=banks[("eq", g, j)][:, 128 * lo : 128 * hi, :, :],
+                in1=by_word(recip[g][:, lo:hi, :].rearrange("p s c -> p (s c)")),
                 op=ALU.mult,
             )
-            x_grouped[(g, j)] = xg
 
         def quantise_x(g, j):
             cols = slice(256 * g, 256 * g + 256)
@@ -186,11 +190,13 @@ def tile_ryeelman_pa_kernel(
             )
 
         def inv_bank(g, k):
-            words = inv_sb[g][:].bitcast(F32)
+            source = inv_sb[g // 2][min(k, 1)]
+            lo = 256 * max(k - 1, 0)
+            words = source[:].bitcast(F32)
             bank = ahead.tile([P, 2, 2, P], F32, tag="ahead")
             for u in range(2):
                 for s in range(2):
-                    nc.tensor.transpose(bank[:, u, s, :], words[:, s, 256 * k + u : 256 * k + 256 : 2], ident[:])
+                    nc.tensor.transpose(bank[:, u, s, :], words[:, 2 * (g % 2) + s, lo + u : lo + 256 : 2], ident[:])
             banks[("inv", g, k)] = bank[:].rearrange("p u s b -> p (s b) u")
 
         def copy_inv(g, k):
@@ -217,23 +223,23 @@ def tile_ryeelman_pa_kernel(
                 stop=stop,
             )
 
-        def products(r):
+        def right_product(r, j):
             g, quarter = ORDER[r]
-            copies = []
-            for j in range(3):
-                right = ring.tile([P, 2, 256], F32, tag="ring")
-                for i in range(2):
-                    mx(right[:, i, :], W_R, 2 * quarter + i, x_codes, x_scales, j, g, True, True)
-                right_sb = block.tile([P, 2, 256], F32, tag="right", bufs=4)
-                nc.scalar.copy(out=right_sb[:], in_=right[:])
-                copies.append(right_sb)
-            for j in range(3):
-                left = ring.tile([P, 2, 256], F32, tag="ring")
-                for i in range(2):
-                    mx(left[:, i, :], W_L, 2 * quarter + i, x_codes, x_scales, j, g, True, True)
-                term = block.tile([P, 2, 256], F32, tag="term%d" % j, bufs=6)
-                nc.vector.tensor_tensor(out=term[:], in0=left[:], in1=copies[j][:], op=ALU.mult)
-                terms[(r, j)] = term
+            right = ring.tile([P, 2, 256], F32, tag="ring")
+            for i in range(2):
+                mx(right[:, i, :], W_R, 2 * quarter + i, x_codes, x_scales, j, g, True, True)
+            right_sb = block.tile([P, 2, 256], F32, tag="right", bufs=7)
+            nc.scalar.copy(out=right_sb[:], in_=right[:])
+            rights[(r, j)] = right_sb
+
+        def left_product(r, j):
+            g, quarter = ORDER[r]
+            left = ring.tile([P, 2, 256], F32, tag="ring")
+            for i in range(2):
+                mx(left[:, i, :], W_L, 2 * quarter + i, x_codes, x_scales, j, g, True, True)
+            term = block.tile([P, 2, 256], F32, tag="term%d" % j, bufs=5)
+            nc.vector.tensor_tensor(out=term[:], in0=left[:], in1=rights[(r, j)][:], op=ALU.mult)
+            terms[(r, j)] = term
 
         def linear(r):
             g, quarter = ORDER[r]
@@ -252,7 +258,7 @@ def tile_ryeelman_pa_kernel(
                 )
 
         def tensor_adds(r):
-            return r < 8 or r >= ROUNDS - 2
+            return r < 3 or r >= ROUNDS - 2
 
         def add_terms(r, j):
             if not tensor_adds(r):
@@ -283,38 +289,40 @@ def tile_ryeelman_pa_kernel(
         with nc.allow_non_contiguous_dma(reason="the first 16 channels arrive in short runs"):
             nc.sync.dma_start(out=head_hidden[:, 0:6, 0:15], in_=hidden_rows[:, 0:6, 0:15])
             nc.sync.dma_start(out=head_input[:], in_=equivariant_input.rearrange("(p s) j -> p (s j)", s=8))
-            load_eq(0)
+            load_eq(0, pieces=2)
             nc.scalar.dma_start(out=head_hidden[:, 6:24, 0:15], in_=hidden_rows[:, 6:24, 0:15])
         nc.vector.memset(bias_rows[:], 0.0)
         nc.gpsimd.dma_start(out=bias_rows[0:8, :], in_=b_ii.rearrange("(r c) -> r c", c=P))
-        load_w(W_R, 0)
-        load_w(W_L, 0)
+        load_w(W_R)
+        load_w(W_L)
         load_eq(1)
-        for k in range(3):
-            load_w(W_I + k, 0)
-        load_inv(0)
+        for k in range(2):
+            load_w(W_I + k)
         load_eq(2)
+        load_w(W_I + 2)
+        load_inv(0)
         load_eq(3)
         load_inv(1)
 
         heads(0)
         square(nc.scalar, 0, 0)
         square(nc.vector, 0, 1)
+        for j in range(3):
+            eq_bank(0, j)
         for s in range(2):
-            norm_bank(0, s)
+            norm_bank(0, s, ring, "ring")
             reciprocal(0, s)
         for w in (W_R, W_L):
             regroup_w(w, 0)
-        heads(1)
-        for w in (W_R, W_L):
-            quantise_w(w, 0)
-            load_w(w, 1)
+        for s in range(2):
+            for j in range(3):
+                scale_eq(0, j, slots=(s, s + 1))
+        quantise_w(W_R, 0)
         for j in range(3):
-            eq_bank(0, j)
-        for j in range(3):
-            scale_eq(0, j)
             quantise_x(0, j)
-        norm(1)
+        quantise_w(W_L, 0)
+        heads(1)
+        squares_of(1)
         bias_ps = ring.tile([P, P], BF16, tag="ring")
         nc.tensor.transpose(bias_ps[:], bias_rows[:], ident_bf[:])
         nc.vector.tensor_copy(out=bias[:], in_=bias_ps[:, 0:8])
@@ -322,70 +330,78 @@ def tile_ryeelman_pa_kernel(
         heads(3)
 
         INV_ROUND = {0: 0, 2: 1, 8: 2, 12: 3}
-        X_ROUND = {1: [(1, 0), (1, 1), (1, 2)]}
-        for g in (2, 3):
-            for j in range(3):
-                X_ROUND[4 * g - 3 + j] = [(g, j)]
+        X_ROUND = {4 * g - 4 + j: (g, j) for g in (2, 3) for j in range(3)}
 
         def banks_for(r):
             if r in INV_ROUND:
                 for k in range(3):
                     inv_bank(INV_ROUND[r], k)
-            for g, j in X_ROUND.get(r, []):
-                eq_bank(g, j)
+            if r in X_ROUND:
+                eq_bank(*X_ROUND[r])
 
         def before_products(r):
-            for g, j in X_ROUND.get(r, []):
-                if g > 1:
-                    scale_eq(g, j)
-                    quantise_x(g, j)
+            if r in X_ROUND:
+                scale_eq(*X_ROUND[r])
+                quantise_x(*X_ROUND[r])
 
         def side_work(r):
-            if r in INV_ROUND:
-                for k in range(3):
-                    copy_inv(INV_ROUND[r], k)
             if r == 0:
-                for k in range(3):
-                    regroup_w(W_I + k, 0)
-                    quantise_w(W_I + k, 0)
-                    load_w(W_I + k, 1)
-                load_inv(2)
-                load_inv(3)
-                norm(2)
-            if r == 1:
+                norm(1)
+                for j in range(3):
+                    eq_bank(1, j)
                 for j in range(3):
                     scale_eq(1, j)
                     quantise_x(1, j)
-                norm(3)
+                squares_of(2)
+                banks_for(0)
+            if r in INV_ROUND:
+                for k in range(3):
+                    copy_inv(INV_ROUND[r], k)
+            if r == 1:
+                for k in range(3):
+                    regroup_w(W_I + k, 0)
+                    quantise_w(W_I + k, 0)
+                norm(2)
+                squares_of(3)
             if r == 2:
+                norm(3)
                 for w in (W_R, W_L):
                     regroup_w(w, 1)
                     quantise_w(w, 1)
-            if r == 3:
-                for k in range(3):
-                    regroup_w(W_I + k, 1)
-                    quantise_w(W_I + k, 1)
             if r in INV_ROUND:
                 for k in range(3):
                     quantise_inv(INV_ROUND[r], k)
+            if r == 4:
+                for k in range(3):
+                    regroup_w(W_I + k, 1)
+                    quantise_w(W_I + k, 1)
 
-        for r in range(ROUNDS + 2):
+        def lin_round(v):
+            return min(v + 2, ROUNDS - 1)
+
+        def turn_round(v):
+            return min(v + 3, ROUNDS)
+
+        for j in range(3):
+            right_product(0, j)
+        for r in range(ROUNDS + 1):
             before_products(r)
+            for j in range(3):
+                if r < ROUNDS:
+                    left_product(r, j)
+                if r + 1 < ROUNDS:
+                    right_product(r + 1, j)
             if r < ROUNDS:
-                products(r)
                 add_terms(r, 2)
-            if r == 0:
-                banks_for(0)
-            if 1 <= r <= ROUNDS:
-                linear(r - 1)
-                add_terms(r - 1, 1)
+            for v in range(ROUNDS):
+                if lin_round(v) == r:
+                    linear(v)
+                    add_terms(v, 1)
             side_work(r)
-            due = [v for v in range(ROUNDS) if v + 2 == r]
-            for v in due[:-1]:
-                turn_back(v)
-                finish(v)
-            for v in due[-1:]:
-                turn_back(v)
+            for v in range(ROUNDS):
+                if turn_round(v) == r:
+                    turn_back(v)
             banks_for(r + 1)
-            for v in due[-1:]:
-                finish(v)
+            for v in range(ROUNDS):
+                if turn_round(v) == r:
+                    finish(v)

@@ -304,32 +304,33 @@ def tile_ryeelman_pa_kernel(
         load_eq(3)
         load_inv(1)
 
-        heads(0)
-        square(nc.scalar, 0, 0)
-        square(nc.vector, 0, 1)
-        for j in range(3):
-            eq_bank(0, j)
-        for s in range(2):
-            norm_bank(0, s, ring, "ring")
-            reciprocal(0, s)
-        for w in (W_R, W_L):
-            regroup_w(w, 0)
-        for s in range(2):
+        with tc.manual_schedule():
+            heads(0)
+            square(nc.scalar, 0, 0)
+            square(nc.vector, 0, 1)
             for j in range(3):
-                scale_eq(0, j, slots=(s, s + 1))
-        quantise_w(W_R, 0)
-        for j in range(3):
-            quantise_x(0, j)
-        quantise_w(W_L, 0)
-        heads(1)
-        squares_of(1)
+                eq_bank(0, j)
+            for s in range(2):
+                norm_bank(0, s, ring, "ring")
+                reciprocal(0, s)
+            regroup_w(W_R, 0)
+            for s in range(2):
+                for j in range(3):
+                    scale_eq(0, j, slots=(s, s + 1))
+            heads(1)
+            quantise_w(W_R, 0)
+            for j in range(3):
+                quantise_x(0, j)
+            regroup_w(W_L, 0)
+            quantise_w(W_L, 0)
+            squares_of(1)
         bias_ps = ring.tile([P, P], BF16, tag="ring")
         nc.tensor.transpose(bias_ps[:], bias_rows[:], ident_bf[:])
         nc.vector.tensor_copy(out=bias[:], in_=bias_ps[:, 0:8])
         heads(2)
         heads(3)
 
-        INV_ROUND = {0: 0, 2: 1, 8: 2, 12: 3}
+        INV_ROUND = {0: 0, 2: 1, 7: 2, 11: 3}
         X_ROUND = {4 * g - 4 + j: (g, j) for g in (2, 3) for j in range(3)}
 
         def banks_for(r):
@@ -340,9 +341,15 @@ def tile_ryeelman_pa_kernel(
                 eq_bank(*X_ROUND[r])
 
         def before_products(r):
+            if r - 1 in X_ROUND:
+                quantise_x(*X_ROUND[r - 1])
+
+        def behind_products(r):
+            if r - 1 in INV_ROUND:
+                for k in range(3):
+                    quantise_inv(INV_ROUND[r - 1], k)
             if r in X_ROUND:
                 scale_eq(*X_ROUND[r])
-                quantise_x(*X_ROUND[r])
 
         def side_work(r):
             if r == 0:
@@ -368,9 +375,6 @@ def tile_ryeelman_pa_kernel(
                 for w in (W_R, W_L):
                     regroup_w(w, 1)
                     quantise_w(w, 1)
-            if r in INV_ROUND:
-                for k in range(3):
-                    quantise_inv(INV_ROUND[r], k)
             if r == 4:
                 for k in range(3):
                     regroup_w(W_I + k, 1)
@@ -393,6 +397,7 @@ def tile_ryeelman_pa_kernel(
                     right_product(r + 1, j)
             if r < ROUNDS:
                 add_terms(r, 2)
+            behind_products(r)
             for v in range(ROUNDS):
                 if lin_round(v) == r:
                     linear(v)

@@ -73,6 +73,12 @@ def tile_ryeelman_pa_kernel(
         eq_sb, inv_sb, w_raw, w_grouped = {}, {}, {}, {}
         banks, squares, recip, x_grouped, i_grouped, terms, turned, rights = {}, {}, {}, {}, {}, {}, {}, {}
 
+        def load_heads(g):
+            with nc.allow_non_contiguous_dma(reason="the first 16 channels arrive in short runs"):
+                nc.sync.dma_start(
+                    out=head_hidden[:, 6 * g : 6 * g + 6, 0:15], in_=hidden_rows[:, 6 * g : 6 * g + 6, 0:15]
+                )
+
         def load_eq(g, pieces=1):
             eq = acts.tile([P, 6, 512], BF16, tag="eq", align_bytes=64)
             n = 6 // pieces
@@ -287,20 +293,22 @@ def tile_ryeelman_pa_kernel(
             nc.sync.dma_start(out=out_rows[:, 2 * g : 2 * g + 2, 256 * quarter : 256 * quarter + 256], in_=res[:])
 
         with nc.allow_non_contiguous_dma(reason="the first 16 channels arrive in short runs"):
-            nc.sync.dma_start(out=head_hidden[:, 0:6, 0:15], in_=hidden_rows[:, 0:6, 0:15])
+            load_heads(0)
             nc.sync.dma_start(out=head_input[:], in_=equivariant_input.rearrange("(p s) j -> p (s j)", s=8))
             load_eq(0, pieces=2)
-            nc.scalar.dma_start(out=head_hidden[:, 6:24, 0:15], in_=hidden_rows[:, 6:24, 0:15])
         nc.vector.memset(bias_rows[:], 0.0)
         nc.gpsimd.dma_start(out=bias_rows[0:8, :], in_=b_ii.rearrange("(r c) -> r c", c=P))
         load_w(W_R)
         load_w(W_L)
+        load_heads(1)
         load_eq(1)
         for k in range(2):
             load_w(W_I + k)
+        load_heads(2)
         load_eq(2)
         load_w(W_I + 2)
         load_inv(0)
+        load_heads(3)
         load_eq(3)
         load_inv(1)
 
@@ -314,22 +322,16 @@ def tile_ryeelman_pa_kernel(
                 norm_bank(0, s, ring, "ring")
                 reciprocal(0, s)
             regroup_w(W_R, 0)
+            quantise_w(W_R, 0)
             for s in range(2):
                 for j in range(3):
                     scale_eq(0, j, slots=(s, s + 1))
             heads(1)
-            quantise_w(W_R, 0)
             for j in range(3):
                 quantise_x(0, j)
             regroup_w(W_L, 0)
             quantise_w(W_L, 0)
             squares_of(1)
-        bias_ps = ring.tile([P, P], BF16, tag="ring")
-        nc.tensor.transpose(bias_ps[:], bias_rows[:], ident_bf[:])
-        nc.vector.tensor_copy(out=bias[:], in_=bias_ps[:, 0:8])
-        heads(2)
-        heads(3)
-
         INV_ROUND = {0: 0, 2: 1, 7: 2, 11: 3}
         X_ROUND = {4 * g - 4 + j: (g, j) for g in (2, 3) for j in range(3)}
 
@@ -359,16 +361,21 @@ def tile_ryeelman_pa_kernel(
                 for j in range(3):
                     scale_eq(1, j)
                     quantise_x(1, j)
+                heads(2)
                 squares_of(2)
                 banks_for(0)
             if r in INV_ROUND:
                 for k in range(3):
                     copy_inv(INV_ROUND[r], k)
             if r == 1:
+                bias_ps = ring.tile([P, P], BF16, tag="ring")
+                nc.tensor.transpose(bias_ps[:], bias_rows[:], ident_bf[:])
+                nc.vector.tensor_copy(out=bias[:], in_=bias_ps[:, 0:8])
                 for k in range(3):
                     regroup_w(W_I + k, 0)
                     quantise_w(W_I + k, 0)
                 norm(2)
+                heads(3)
                 squares_of(3)
             if r == 2:
                 norm(3)

@@ -39,8 +39,8 @@ def tile_ryeelman_pa_kernel(
         work = ctx.enter_context(tc.tile_pool(name="work", bufs=2))
         stage = ctx.enter_context(tc.tile_pool(name="stage", bufs=2))
         block = ctx.enter_context(tc.tile_pool(name="block", bufs=3))
-        ahead = ctx.enter_context(tc.psum_pool(name="ahead", bufs=3))
-        ring = ctx.enter_context(tc.psum_pool(name="ring", bufs=5))
+        ahead = ctx.enter_context(tc.psum_pool(name="ahead", bufs=2))
+        ring = ctx.enter_context(tc.psum_pool(name="ring", bufs=6))
 
         zero = keep.tile([P, 1], F32)
         nc.vector.memset(zero[:], 0.0)
@@ -169,9 +169,9 @@ def tile_ryeelman_pa_kernel(
             for s in range(2):
                 reciprocal(g, s)
 
-        def eq_bank(g, j):
+        def eq_bank(g, j, pool=ahead, tag="ahead"):
             words = eq_sb[g][:].bitcast(F32)
-            bank = ahead.tile([P, 2, 2, P], F32, tag="ahead")
+            bank = pool.tile([P, 2, 2, P], F32, tag=tag)
             for u in range(2):
                 for s in range(2):
                     nc.tensor.transpose(bank[:, u, s, :], words[:, 3 * s + j, u::2], ident[:])
@@ -270,27 +270,34 @@ def tile_ryeelman_pa_kernel(
             if not tensor_adds(r):
                 nc.gpsimd.tensor_tensor(out=terms[(r, j - 1)][:], in0=terms[(r, j - 1)][:], in1=terms[(r, j)][:], op=ALU.add)
 
+        def slot_runs(r):
+            return ((0, 2),) if r < ROUNDS - 1 else ((0, 1), (1, 2))
+
         def turn_back(r):
-            bank = ring.tile([P, 2, 2, P], F32, tag="ring")
             n_terms = 3 if tensor_adds(r) else 1
-            for s in range(2):
-                for i in range(2):
-                    for j in range(n_terms):
-                        nc.tensor.matmul(
-                            out=bank[:, s, i, :],
-                            lhsT=terms[(r, j)][:, i, 128 * s : 128 * s + 128],
-                            rhs=ident[:],
-                            is_transpose=True,
-                            start=(j == 0),
-                            stop=(j == n_terms - 1),
-                        )
-            turned[r] = bank
+            for lo, hi in slot_runs(r):
+                bank = ring.tile([P, hi - lo, 2, P], F32, tag="ring")
+                for s in range(lo, hi):
+                    for i in range(2):
+                        for j in range(n_terms):
+                            nc.tensor.matmul(
+                                out=bank[:, s - lo, i, :],
+                                lhsT=terms[(r, j)][:, i, 128 * s : 128 * s + 128],
+                                rhs=ident[:],
+                                is_transpose=True,
+                                start=(j == 0),
+                                stop=(j == n_terms - 1),
+                            )
+                turned[(r, lo)] = bank
 
         def finish(r):
             g, quarter = ORDER[r]
-            res = block.tile([P, 2, 256], F32, tag="res")
-            nc.scalar.activation(out=res[:], in_=turned[r][:].rearrange("p s i h -> p s (i h)"), func=ACT.Tanh)
-            nc.sync.dma_start(out=out_rows[:, 2 * g : 2 * g + 2, 256 * quarter : 256 * quarter + 256], in_=res[:])
+            for lo, hi in slot_runs(r):
+                res = block.tile([P, hi - lo, 256], F32, tag="res")
+                nc.scalar.activation(out=res[:], in_=turned[(r, lo)][:].rearrange("p s i h -> p s (i h)"), func=ACT.Tanh)
+                nc.sync.dma_start(
+                    out=out_rows[:, 2 * g + lo : 2 * g + hi, 256 * quarter : 256 * quarter + 256], in_=res[:]
+                )
 
         with nc.allow_non_contiguous_dma(reason="the first 16 channels arrive in short runs"):
             load_heads(0)
@@ -316,8 +323,9 @@ def tile_ryeelman_pa_kernel(
             heads(0)
             square(nc.scalar, 0, 0)
             square(nc.vector, 0, 1)
-            for j in range(3):
+            for j in range(2):
                 eq_bank(0, j)
+            eq_bank(0, 2, ring, "ring")
             for s in range(2):
                 norm_bank(0, s, ring, "ring")
                 reciprocal(0, s)
@@ -337,7 +345,7 @@ def tile_ryeelman_pa_kernel(
 
         def banks_for(r):
             if r in INV_ROUND:
-                for k in range(3):
+                for k in range(2):
                     inv_bank(INV_ROUND[r], k)
             if r in X_ROUND:
                 eq_bank(*X_ROUND[r])
@@ -356,16 +364,22 @@ def tile_ryeelman_pa_kernel(
         def side_work(r):
             if r == 0:
                 norm(1)
-                for j in range(3):
+                for j in range(2):
                     eq_bank(1, j)
-                for j in range(3):
-                    scale_eq(1, j)
+                scale_eq(1, 0)
+                eq_bank(1, 2)
+                scale_eq(1, 1)
+                quantise_x(1, 0)
+                scale_eq(1, 2)
+                for j in range(1, 3):
                     quantise_x(1, j)
                 heads(2)
                 squares_of(2)
                 banks_for(0)
             if r in INV_ROUND:
-                for k in range(3):
+                copy_inv(INV_ROUND[r], 0)
+                inv_bank(INV_ROUND[r], 2)
+                for k in range(1, 3):
                     copy_inv(INV_ROUND[r], k)
             if r == 1:
                 bias_ps = ring.tile([P, P], BF16, tag="ring")
@@ -387,11 +401,19 @@ def tile_ryeelman_pa_kernel(
                     regroup_w(W_I + k, 1)
                     quantise_w(W_I + k, 1)
 
+        CATCH_UP = 11
+
         def lin_round(v):
-            return min(v + 2, ROUNDS - 1)
+            return min(v + (2 if v < CATCH_UP else 1), ROUNDS - 1)
 
         def turn_round(v):
-            return min(v + 3, ROUNDS)
+            return lin_round(v) + 1
+
+        def linear_parts(r):
+            for v in range(ROUNDS):
+                if lin_round(v) == r:
+                    linear(v)
+                    add_terms(v, 1)
 
         for j in range(3):
             right_product(0, j)
@@ -402,13 +424,13 @@ def tile_ryeelman_pa_kernel(
                     left_product(r, j)
                 if r + 1 < ROUNDS:
                     right_product(r + 1, j)
+                if r == ROUNDS - 1 and j == 0:
+                    linear_parts(r)
             if r < ROUNDS:
                 add_terms(r, 2)
             behind_products(r)
-            for v in range(ROUNDS):
-                if lin_round(v) == r:
-                    linear(v)
-                    add_terms(v, 1)
+            if r < ROUNDS - 1:
+                linear_parts(r)
             side_work(r)
             for v in range(ROUNDS):
                 if turn_round(v) == r:

@@ -264,7 +264,7 @@ def tile_ryeelman_pa_kernel(
                 )
 
         def tensor_adds(r):
-            return r < 3 or r >= ROUNDS - 2
+            return r < 1 or r >= ROUNDS - 2
 
         def add_terms(r, j):
             if not tensor_adds(r):
@@ -432,10 +432,10 @@ def tile_ryeelman_pa_kernel(
             if r < ROUNDS - 1:
                 linear_parts(r)
             side_work(r)
+            banks_for(r + 1)
             for v in range(ROUNDS):
                 if turn_round(v) == r:
                     turn_back(v)
-            banks_for(r + 1)
             for v in range(ROUNDS):
                 if turn_round(v) == r:
                     finish(v)

@@ -268,7 +268,9 @@ def tile_ryeelman_pa_kernel(
 
         def add_terms(r, j):
             if not tensor_adds(r):
-                nc.gpsimd.tensor_tensor(out=terms[(r, j - 1)][:], in0=terms[(r, j - 1)][:], in1=terms[(r, j)][:], op=ALU.add)
+                for i in range(2):
+                    total, term = terms[(r, j - 1)][:, i, :], terms[(r, j)][:, i, :]
+                    nc.gpsimd.tensor_tensor(out=total, in0=total, in1=term, op=ALU.add)
 
         def slot_runs(r):
             return ((0, 2),) if r < ROUNDS - 1 else ((0, 1), (1, 2))

@@ -39,8 +39,7 @@ def tile_ryeelman_pa_kernel(
         work = ctx.enter_context(tc.tile_pool(name="work", bufs=2))
         stage = ctx.enter_context(tc.tile_pool(name="stage", bufs=2))
         block = ctx.enter_context(tc.tile_pool(name="block", bufs=3))
-        ahead = ctx.enter_context(tc.psum_pool(name="ahead", bufs=2))
-        ring = ctx.enter_context(tc.psum_pool(name="ring", bufs=6))
+        ring = ctx.enter_context(tc.psum_pool(name="ring", bufs=8))
 
         zero = keep.tile([P, 1], F32)
         nc.vector.memset(zero[:], 0.0)
@@ -57,12 +56,12 @@ def tile_ryeelman_pa_kernel(
         head_input = keep.tile([P, 24], BF16)
         bias_rows = keep.tile([P, P], BF16)
         bias = keep.tile([P, 8], F32)
-        w_codes = keep.tile([P, 5, 1024], U32, align_bytes=64)
-        w_scales = keep.tile([P, 5, 1024], U8, align_bytes=64)
-        x_codes = keep.tile([P, 3, 1024], U32, align_bytes=64)
-        x_scales = keep.tile([P, 3, 1024], U8, align_bytes=64)
-        i_codes = keep.tile([P, 3, 1024], U32, align_bytes=64)
-        i_scales = keep.tile([P, 3, 1024], U8, align_bytes=64)
+        w_codes = keep.tile([P, 2, 5, 512], U32, align_bytes=64)
+        w_scales = keep.tile([P, 2, 5, 512], U8, align_bytes=64)
+        x_codes = keep.tile([P, GROUPS, 3, 256], U32, align_bytes=64)
+        x_scales = keep.tile([P, GROUPS, 3, 256], U8, align_bytes=64)
+        i_codes = keep.tile([P, GROUPS, 3, 256], U32, align_bytes=64)
+        i_scales = keep.tile([P, GROUPS, 3, 256], U8, align_bytes=64)
 
         hidden_rows = equivariant_hidden.rearrange("(p s) j c -> p (s j) c", s=8)
         input_rows = invariant_input.rearrange("(p s) c -> p s c", s=8)
@@ -70,7 +69,7 @@ def tile_ryeelman_pa_kernel(
         out_rows = out.rearrange("(p s) h -> p s h", s=8)
         w_hbm = (W_right, W_left, W_ii[0:512, :], W_ii[512:1024, :], W_ii[1024:1536, :])
 
-        eq_sb, inv_sb, w_raw, w_grouped = {}, {}, {}, {}
+        eq_sb, inv_sb, w_raw = {}, {}, {}
         banks, squares, recip, x_grouped, i_grouped, terms, turned, rights = {}, {}, {}, {}, {}, {}, {}, {}
 
         def load_heads(g):
@@ -87,8 +86,9 @@ def tile_ryeelman_pa_kernel(
             eq_sb[g] = eq
 
         def heads(g):
-            nc.vector.tensor_copy(out=eq_sb[g][:, :, 1:16], in_=head_hidden[:, 6 * g : 6 * g + 6, 0:15])
-            nc.vector.tensor_copy(out=eq_sb[g][:, :, 0:1], in_=head_input[:, 6 * g : 6 * g + 6].unsqueeze(2))
+            engine = nc.vector if g == 0 else nc.gpsimd
+            engine.tensor_copy(out=eq_sb[g][:, :, 1:16], in_=head_hidden[:, 6 * g : 6 * g + 6, 0:15])
+            engine.tensor_copy(out=eq_sb[g][:, :, 0:1], in_=head_input[:, 6 * g : 6 * g + 6].unsqueeze(2))
 
         def load_inv(pair):
             first = acts.tile([P, 4, 512], BF16, tag="inv_input", bufs=2, align_bytes=64)
@@ -102,20 +102,21 @@ def tile_ryeelman_pa_kernel(
             nc.sync.dma_start(out=raw[:], in_=w_hbm[w].rearrange("(p t) c -> p t c", t=4))
             w_raw[w] = raw
 
-        def regroup_w(w, half):
-            grouped = stage.tile([P, 512, 4], BF16, tag="grouped", align_bytes=64)
-            nc.vector.tensor_copy(
-                out=grouped[:].rearrange("p (c i) t -> p c t i", i=4),
-                in_=w_raw[w][:, :, 512 * half : 512 * half + 512].rearrange("p t (c i) -> p c t i", i=4),
-            )
-            w_grouped[(w, half)] = grouped
+        def flat(ap):
+            return ap.rearrange("p a b -> p (a b)")
 
-        def quantise_w(w, half):
-            cols = slice(512 * half, 512 * half + 512)
+        def prepare_w(ws, half):
+            n = len(ws)
+            grouped = stage.tile([P, n, 512, 4], BF16, tag="grouped", align_bytes=64)
+            for i, w in enumerate(ws):
+                nc.vector.tensor_copy(
+                    out=grouped[:, i, :, :].rearrange("p (c i) t -> p c t i", i=4),
+                    in_=w_raw[w][:, :, 512 * half : 512 * half + 512].rearrange("p t (c i) -> p c t i", i=4),
+                )
             nc.vector.quantize_mx(
-                out=w_codes[:, w, cols].bitcast(FP8X4),
-                scales=w_scales[:, w, cols],
-                in_=w_grouped[(w, half)][:].rearrange("p c t -> p (c t)"),
+                out=flat(w_codes[:, half, ws[0] : ws[0] + n, :]).bitcast(FP8X4),
+                scales=flat(w_scales[:, half, ws[0] : ws[0] + n, :]),
+                in_=grouped[:].rearrange("p n c t -> p (n c t)"),
             )
 
         def by_word(ap):
@@ -132,8 +133,8 @@ def tile_ryeelman_pa_kernel(
                 else:
                     nc.vector.tensor_tensor(out=dst, in0=src, in1=src, op=ALU.mult)
 
-        def norm_bank(g, s, pool=ahead, tag="ahead"):
-            bank = pool.tile([P, 4, P], F32, tag=tag)
+        def norm_bank(g, s):
+            bank = ring.tile([P, 4, P], F32, tag="ring")
             for t in range(4):
                 for j in range(3):
                     nc.tensor.matmul(
@@ -169,62 +170,65 @@ def tile_ryeelman_pa_kernel(
             for s in range(2):
                 reciprocal(g, s)
 
-        def eq_bank(g, j, pool=ahead, tag="ahead"):
+        def eq_bank(g, j):
             words = eq_sb[g][:].bitcast(F32)
-            bank = pool.tile([P, 2, 2, P], F32, tag=tag)
+            bank = ring.tile([P, 2, 2, P], F32, tag="ring")
             for u in range(2):
                 for s in range(2):
                     nc.tensor.transpose(bank[:, u, s, :], words[:, 3 * s + j, u::2], ident[:])
             banks[("eq", g, j)] = bank[:].bitcast(BF16).rearrange("p u s (b e) -> p (s b) u e", e=2)
 
         def scale_eq(g, j, slots=(0, 2)):
-            if (g, j) not in x_grouped:
-                xg = work.tile([P, 1024], BF16, tag="x_grouped", bufs=3, align_bytes=64)
-                x_grouped[(g, j)] = xg
+            if g not in x_grouped:
+                xg = work.tile([P, 3, 1024], BF16, tag="x_grouped", bufs=1, align_bytes=64)
+                x_grouped[g] = xg
             lo, hi = slots
             nc.vector.tensor_tensor(
-                out=by_word(x_grouped[(g, j)][:, 512 * lo : 512 * hi]),
+                out=by_word(x_grouped[g][:, j, 512 * lo : 512 * hi]),
                 in0=banks[("eq", g, j)][:, 128 * lo : 128 * hi, :, :],
                 in1=by_word(recip[g][:, lo:hi, :].rearrange("p s c -> p (s c)")),
                 op=ALU.mult,
             )
 
-        def quantise_x(g, j):
-            cols = slice(256 * g, 256 * g + 256)
+        def quantise_x(g, lo, hi):
             nc.vector.quantize_mx(
-                out=x_codes[:, j, cols].bitcast(FP8X4), scales=x_scales[:, j, cols], in_=x_grouped[(g, j)][:]
+                out=flat(x_codes[:, g, lo:hi, :]).bitcast(FP8X4),
+                scales=flat(x_scales[:, g, lo:hi, :]),
+                in_=flat(x_grouped[g][:, lo:hi, :]),
             )
 
         def inv_bank(g, k):
             source = inv_sb[g // 2][min(k, 1)]
             lo = 256 * max(k - 1, 0)
             words = source[:].bitcast(F32)
-            bank = ahead.tile([P, 2, 2, P], F32, tag="ahead")
+            bank = ring.tile([P, 2, 2, P], F32, tag="ring")
             for u in range(2):
                 for s in range(2):
                     nc.tensor.transpose(bank[:, u, s, :], words[:, 2 * (g % 2) + s, lo + u : lo + 256 : 2], ident[:])
             banks[("inv", g, k)] = bank[:].rearrange("p u s b -> p (s b) u")
 
         def copy_inv(g, k):
-            ig = work.tile([P, 1024], BF16, tag="i_grouped", bufs=3, align_bytes=64)
-            nc.scalar.copy(out=ig[:].bitcast(F32).rearrange("p (b u) -> p b u", u=2), in_=banks[("inv", g, k)])
-            i_grouped[(g, k)] = ig
+            if g not in i_grouped:
+                ig = work.tile([P, 3, 1024], BF16, tag="i_grouped", bufs=1, align_bytes=64)
+                i_grouped[g] = ig
+            nc.scalar.copy(out=i_grouped[g][:, k, :].bitcast(F32).rearrange("p (b u) -> p b u", u=2), in_=banks[("inv", g, k)])
 
-        def quantise_inv(g, k):
-            cols = slice(256 * g, 256 * g + 256)
+        def quantise_inv(g, lo, hi):
             nc.vector.quantize_mx(
-                out=i_codes[:, k, cols].bitcast(FP8X4), scales=i_scales[:, k, cols], in_=i_grouped[(g, k)][:]
+                out=flat(i_codes[:, g, lo:hi, :]).bitcast(FP8X4),
+                scales=flat(i_scales[:, g, lo:hi, :]),
+                in_=flat(i_grouped[g][:, lo:hi, :]),
             )
 
         def mx(acc, w, h_tile, codes, scales, row, g, start, stop):
-            h_cols = slice(128 * h_tile, 128 * h_tile + 128)
-            b_cols = slice(256 * g, 256 * g + 256)
+            half, tile_of_half = divmod(h_tile, 4)
+            h_cols = slice(128 * tile_of_half, 128 * tile_of_half + 128)
             nc.tensor.matmul_mx(
                 out=acc,
-                lhsT=w_codes[:, w, h_cols].bitcast(FP8X4),
-                lhsT_scale=w_scales[:, w, h_cols],
-                rhs=codes[:, row, b_cols].bitcast(FP8X4),
-                rhs_scale=scales[:, row, b_cols],
+                lhsT=w_codes[:, half, w, h_cols].bitcast(FP8X4),
+                lhsT_scale=w_scales[:, half, w, h_cols],
+                rhs=codes[:, g, row, :].bitcast(FP8X4),
+                rhs_scale=scales[:, g, row, :],
                 start=start,
                 stop=stop,
             )
@@ -234,7 +238,7 @@ def tile_ryeelman_pa_kernel(
             right = ring.tile([P, 2, 256], F32, tag="ring")
             for i in range(2):
                 mx(right[:, i, :], W_R, 2 * quarter + i, x_codes, x_scales, j, g, True, True)
-            right_sb = block.tile([P, 2, 256], F32, tag="right", bufs=7)
+            right_sb = block.tile([P, 2, 256], F32, tag="right", bufs=6)
             nc.scalar.copy(out=right_sb[:], in_=right[:])
             rights[(r, j)] = right_sb
 
@@ -325,22 +329,19 @@ def tile_ryeelman_pa_kernel(
             heads(0)
             square(nc.scalar, 0, 0)
             square(nc.vector, 0, 1)
-            for j in range(2):
+            for j in range(3):
                 eq_bank(0, j)
-            eq_bank(0, 2, ring, "ring")
             for s in range(2):
-                norm_bank(0, s, ring, "ring")
+                norm_bank(0, s)
                 reciprocal(0, s)
-            regroup_w(W_R, 0)
-            quantise_w(W_R, 0)
+            prepare_w((W_R,), 0)
             for s in range(2):
                 for j in range(3):
                     scale_eq(0, j, slots=(s, s + 1))
             heads(1)
-            for j in range(3):
-                quantise_x(0, j)
-            regroup_w(W_L, 0)
-            quantise_w(W_L, 0)
+            quantise_x(0, 0, 1)
+            quantise_x(0, 1, 3)
+            prepare_w((W_L,), 0)
             squares_of(1)
         INV_ROUND = {0: 0, 2: 1, 7: 2, 11: 3}
         X_ROUND = {4 * g - 4 + j: (g, j) for g in (2, 3) for j in range(3)}
@@ -353,13 +354,14 @@ def tile_ryeelman_pa_kernel(
                 eq_bank(*X_ROUND[r])
 
         def before_products(r):
-            if r - 1 in X_ROUND:
-                quantise_x(*X_ROUND[r - 1])
+            if r - 1 in X_ROUND and X_ROUND[r - 1][1] > 0:
+                g, j = X_ROUND[r - 1]
+                quantise_x(g, 2 * j - 2, j + 1)
 
         def behind_products(r):
             if r - 1 in INV_ROUND:
-                for k in range(3):
-                    quantise_inv(INV_ROUND[r - 1], k)
+                quantise_inv(INV_ROUND[r - 1], 0, 2)
+                quantise_inv(INV_ROUND[r - 1], 2, 3)
             if r in X_ROUND:
                 scale_eq(*X_ROUND[r])
 
@@ -371,10 +373,9 @@ def tile_ryeelman_pa_kernel(
                 scale_eq(1, 0)
                 eq_bank(1, 2)
                 scale_eq(1, 1)
-                quantise_x(1, 0)
                 scale_eq(1, 2)
-                for j in range(1, 3):
-                    quantise_x(1, j)
+                quantise_x(1, 0, 2)
+                quantise_x(1, 2, 3)
                 heads(2)
                 squares_of(2)
                 banks_for(0)
@@ -387,21 +388,17 @@ def tile_ryeelman_pa_kernel(
                 bias_ps = ring.tile([P, P], BF16, tag="ring")
                 nc.tensor.transpose(bias_ps[:], bias_rows[:], ident_bf[:])
                 nc.vector.tensor_copy(out=bias[:], in_=bias_ps[:, 0:8])
-                for k in range(3):
-                    regroup_w(W_I + k, 0)
-                    quantise_w(W_I + k, 0)
+                prepare_w((W_I, W_I + 1), 0)
+                prepare_w((W_I + 2,), 0)
                 norm(2)
                 heads(3)
                 squares_of(3)
             if r == 2:
                 norm(3)
-                for w in (W_R, W_L):
-                    regroup_w(w, 1)
-                    quantise_w(w, 1)
+                prepare_w((W_R, W_L), 1)
             if r == 4:
-                for k in range(3):
-                    regroup_w(W_I + k, 1)
-                    quantise_w(W_I + k, 1)
+                prepare_w((W_I, W_I + 1), 1)
+                prepare_w((W_I + 2,), 1)
 
         CATCH_UP = 11
 

@@ -268,7 +268,7 @@ def tile_ryeelman_pa_kernel(
                 )
 
         def tensor_adds(r):
-            return r < 1 or r >= ROUNDS - 2
+            return r >= ROUNDS - 2
 
         def add_terms(r, j):
             if not tensor_adds(r):
@@ -315,10 +315,10 @@ def tile_ryeelman_pa_kernel(
         load_w(W_L)
         load_heads(1)
         load_eq(1)
-        for k in range(2):
-            load_w(W_I + k)
         load_heads(2)
         load_eq(2)
+        load_w(W_I)
+        load_w(W_I + 1)
         load_w(W_I + 2)
         load_inv(0)
         load_heads(3)
@@ -343,12 +343,12 @@ def tile_ryeelman_pa_kernel(
             quantise_x(0, 1, 3)
             prepare_w((W_L,), 0)
             squares_of(1)
-        INV_ROUND = {0: 0, 2: 1, 7: 2, 11: 3}
+        INV_ROUND = {0: 0, 1: 1, 7: 2, 11: 3}
         X_ROUND = {4 * g - 4 + j: (g, j) for g in (2, 3) for j in range(3)}
 
         def banks_for(r):
             if r in INV_ROUND:
-                for k in range(2):
+                for k in range(3):
                     inv_bank(INV_ROUND[r], k)
             if r in X_ROUND:
                 eq_bank(*X_ROUND[r])
@@ -368,42 +368,38 @@ def tile_ryeelman_pa_kernel(
         def side_work(r):
             if r == 0:
                 norm(1)
-                for j in range(2):
+                for j in range(3):
                     eq_bank(1, j)
-                scale_eq(1, 0)
-                eq_bank(1, 2)
-                scale_eq(1, 1)
-                scale_eq(1, 2)
+                for j in range(3):
+                    scale_eq(1, j)
                 quantise_x(1, 0, 2)
                 quantise_x(1, 2, 3)
                 heads(2)
                 squares_of(2)
                 banks_for(0)
             if r in INV_ROUND:
-                copy_inv(INV_ROUND[r], 0)
-                inv_bank(INV_ROUND[r], 2)
-                for k in range(1, 3):
+                for k in range(3):
                     copy_inv(INV_ROUND[r], k)
-            if r == 1:
+            if r == 2:
                 bias_ps = ring.tile([P, P], BF16, tag="ring")
                 nc.tensor.transpose(bias_ps[:], bias_rows[:], ident_bf[:])
                 nc.vector.tensor_copy(out=bias[:], in_=bias_ps[:, 0:8])
+            if r == 0:
                 prepare_w((W_I, W_I + 1), 0)
+                prepare_w((W_R, W_L), 1)
+            if r == 1:
                 prepare_w((W_I + 2,), 0)
                 norm(2)
                 heads(3)
                 squares_of(3)
             if r == 2:
                 norm(3)
-                prepare_w((W_R, W_L), 1)
-            if r == 4:
                 prepare_w((W_I, W_I + 1), 1)
+            if r == 4:
                 prepare_w((W_I + 2,), 1)
 
-        CATCH_UP = 11
-
         def lin_round(v):
-            return min(v + (2 if v < CATCH_UP else 1), ROUNDS - 1)
+            return min(v + (3 if v < 8 else 1 if v < 14 else 0), ROUNDS - 1)
 
         def turn_round(v):
             return lin_round(v) + 1
@@ -423,13 +419,11 @@ def tile_ryeelman_pa_kernel(
                     left_product(r, j)
                 if r + 1 < ROUNDS:
                     right_product(r + 1, j)
-                if r == ROUNDS - 1 and j == 0:
+                if j == (1 if r < ROUNDS - 1 else 0):
                     linear_parts(r)
             if r < ROUNDS:
                 add_terms(r, 2)
             behind_products(r)
-            if r < ROUNDS - 1:
-                linear_parts(r)
             side_work(r)
             banks_for(r + 1)
             for v in range(ROUNDS):

@@ -107,7 +107,7 @@ def tile_ryeelman_pa_kernel(
 
         def prepare_w(ws, half):
             n = len(ws)
-            grouped = stage.tile([P, n, 512, 4], BF16, tag="grouped", align_bytes=64)
+            grouped = stage.tile([P, n, 512, 4], BF16, tag="grouped%d" % n, bufs=1, align_bytes=64)
             for i, w in enumerate(ws):
                 nc.vector.tensor_copy(
                     out=grouped[:, i, :, :].rearrange("p (c i) t -> p c t i", i=4),
@@ -268,7 +268,7 @@ def tile_ryeelman_pa_kernel(
                 )
 
         def tensor_adds(r):
-            return r >= ROUNDS - 2
+            return r < 1 or r >= ROUNDS - 2
 
         def add_terms(r, j):
             if not tensor_adds(r):
@@ -299,7 +299,7 @@ def tile_ryeelman_pa_kernel(
         def finish(r):
             g, quarter = ORDER[r]
             for lo, hi in slot_runs(r):
-                res = block.tile([P, hi - lo, 256], F32, tag="res")
+                res = block.tile([P, hi - lo, 256], F32, tag="res", bufs=5)
                 nc.scalar.activation(out=res[:], in_=turned[(r, lo)][:].rearrange("p s i h -> p s (i h)"), func=ACT.Tanh)
                 nc.sync.dma_start(
                     out=out_rows[:, 2 * g + lo : 2 * g + hi, 256 * quarter : 256 * quarter + 256], in_=res[:]
@@ -315,12 +315,12 @@ def tile_ryeelman_pa_kernel(
         load_w(W_L)
         load_heads(1)
         load_eq(1)
-        load_heads(2)
-        load_eq(2)
+        load_inv(0)
         load_w(W_I)
         load_w(W_I + 1)
         load_w(W_I + 2)
-        load_inv(0)
+        load_heads(2)
+        load_eq(2)
         load_heads(3)
         load_eq(3)
         load_inv(1)
@@ -329,41 +329,43 @@ def tile_ryeelman_pa_kernel(
             heads(0)
             square(nc.scalar, 0, 0)
             square(nc.vector, 0, 1)
-            for j in range(3):
-                eq_bank(0, j)
             for s in range(2):
+                eq_bank(0, s)
                 norm_bank(0, s)
                 reciprocal(0, s)
+            eq_bank(0, 2)
             prepare_w((W_R,), 0)
-            for s in range(2):
-                for j in range(3):
-                    scale_eq(0, j, slots=(s, s + 1))
-            heads(1)
+            for j in range(3):
+                scale_eq(0, j, slots=(0, 1))
+            for j in range(2):
+                scale_eq(0, j, slots=(1, 2))
             quantise_x(0, 0, 1)
+            scale_eq(0, 2, slots=(1, 2))
+            heads(1)
             quantise_x(0, 1, 3)
             prepare_w((W_L,), 0)
             squares_of(1)
-        INV_ROUND = {0: 0, 1: 1, 7: 2, 11: 3}
-        X_ROUND = {4 * g - 4 + j: (g, j) for g in (2, 3) for j in range(3)}
+        INV_ROUND = {0: 0, 1: 1, 7: 2, 10: 3}
+        X_ROUND = {3: ((2, 0),), 5: ((2, 1),), 6: ((2, 2),), 7: ((3, 0),), 9: ((3, 1), (3, 2))}
 
         def banks_for(r):
             if r in INV_ROUND:
-                for k in range(3):
+                for k in range(2):
                     inv_bank(INV_ROUND[r], k)
-            if r in X_ROUND:
-                eq_bank(*X_ROUND[r])
+            for g, j in X_ROUND.get(r, ()):
+                eq_bank(g, j)
 
         def before_products(r):
-            if r - 1 in X_ROUND and X_ROUND[r - 1][1] > 0:
-                g, j = X_ROUND[r - 1]
-                quantise_x(g, 2 * j - 2, j + 1)
+            for g, j in X_ROUND.get(r - 1, ()):
+                if j > 0:
+                    quantise_x(g, 2 * j - 2, j + 1)
 
         def behind_products(r):
             if r - 1 in INV_ROUND:
                 quantise_inv(INV_ROUND[r - 1], 0, 2)
                 quantise_inv(INV_ROUND[r - 1], 2, 3)
-            if r in X_ROUND:
-                scale_eq(*X_ROUND[r])
+            for g, j in X_ROUND.get(r, ()):
+                scale_eq(g, j)
 
         def side_work(r):
             if r == 0:
@@ -374,32 +376,32 @@ def tile_ryeelman_pa_kernel(
                     scale_eq(1, j)
                 quantise_x(1, 0, 2)
                 quantise_x(1, 2, 3)
-                heads(2)
-                squares_of(2)
+            if r in (0, 2):
+                heads(2 + r // 2)
+                squares_of(2 + r // 2)
+            if r == 0:
                 banks_for(0)
             if r in INV_ROUND:
                 for k in range(3):
+                    if k == 2:
+                        inv_bank(INV_ROUND[r], k)
                     copy_inv(INV_ROUND[r], k)
-            if r == 2:
+            if r == 1:
                 bias_ps = ring.tile([P, P], BF16, tag="ring")
                 nc.tensor.transpose(bias_ps[:], bias_rows[:], ident_bf[:])
                 nc.vector.tensor_copy(out=bias[:], in_=bias_ps[:, 0:8])
-            if r == 0:
                 prepare_w((W_I, W_I + 1), 0)
-                prepare_w((W_R, W_L), 1)
-            if r == 1:
                 prepare_w((W_I + 2,), 0)
-                norm(2)
-                heads(3)
-                squares_of(3)
+                prepare_w((W_R, W_L), 1)
             if r == 2:
-                norm(3)
+                for g in (2, 3):
+                    norm(g)
                 prepare_w((W_I, W_I + 1), 1)
             if r == 4:
                 prepare_w((W_I + 2,), 1)
 
         def lin_round(v):
-            return min(v + (3 if v < 8 else 1 if v < 14 else 0), ROUNDS - 1)
+            return v + (2 if v < 6 else 1 if v < 14 else 0)
 
         def turn_round(v):
             return lin_round(v) + 1
@@ -415,15 +417,16 @@ def tile_ryeelman_pa_kernel(
         for r in range(ROUNDS + 1):
             before_products(r)
             for j in range(3):
-                if r < ROUNDS:
-                    left_product(r, j)
                 if r + 1 < ROUNDS:
                     right_product(r + 1, j)
+                if r < ROUNDS:
+                    left_product(r, j)
                 if j == (1 if r < ROUNDS - 1 else 0):
                     linear_parts(r)
+                if j == 1:
+                    behind_products(r)
             if r < ROUNDS:
                 add_terms(r, 2)
-            behind_products(r)
             side_work(r)
             banks_for(r + 1)
             for v in range(ROUNDS):

from contextlib import ExitStack

import concourse.mybir as mybir
from concourse.masks import make_identity

F32 = mybir.dt.float32
BF16 = mybir.dt.bfloat16
U32 = mybir.dt.uint32
U8 = mybir.dt.uint8
FP8X4 = mybir.dt.float8_e4m3fn_x4
ACT = mybir.ActivationFunctionType
ALU = mybir.AluOpType

FLOPS = 2 * (2 * 3072 * 512 * 1024 + 1024 * 1536 * 1024)
EPS = 1e-6
P = 128
GROUPS = 4
ORDER = [(g, q) for half in ((0, 1), (2, 3)) for g in (0, 1) for q in half] + [(g, q) for g in (2, 3) for q in range(4)]
ROUNDS = len(ORDER)
W_R, W_L, W_I = 0, 1, 2


def tile_ryeelman_pa_kernel(
    tc,
    invariant_input,
    equivariant_input,
    invariant_hidden,
    equivariant_hidden,
    W_left,
    W_right,
    W_ii,
    b_ii,
    out,
):
    nc = tc.nc
    with ExitStack() as ctx:
        keep = ctx.enter_context(tc.tile_pool(name="keep", bufs=1))
        acts = ctx.enter_context(tc.tile_pool(name="acts", bufs=3))
        work = ctx.enter_context(tc.tile_pool(name="work", bufs=2))
        stage = ctx.enter_context(tc.tile_pool(name="stage", bufs=2))
        block = ctx.enter_context(tc.tile_pool(name="block", bufs=3))
        ring = ctx.enter_context(tc.psum_pool(name="ring", bufs=8))

        zero = keep.tile([P, 1], F32)
        nc.vector.memset(zero[:], 0.0)
        eps = keep.tile([P, 1], F32)
        nc.vector.tensor_scalar_add(out=eps[:], in0=zero[:], scalar1=EPS)
        warm = keep.tile([P, 1], F32)
        nc.scalar.activation(out=warm[:], in_=eps[:], func=ACT.Abs_reciprocal_sqrt)
        ident = keep.tile([P, P], F32)
        make_identity(nc, ident[:])
        ident_bf = keep.tile([P, P], BF16)
        make_identity(nc, ident_bf[:])

        head_hidden = keep.tile([P, 24, 16], BF16)
        head_input = keep.tile([P, 24], BF16)
        bias_rows = keep.tile([P, P], BF16)
        bias = keep.tile([P, 8], F32)
        w_codes = keep.tile([P, 2, 5, 512], U32, align_bytes=64)
        w_scales = keep.tile([P, 2, 5, 512], U8, align_bytes=64)
        x_codes = keep.tile([P, GROUPS, 3, 256], U32, align_bytes=64)
        x_scales = keep.tile([P, GROUPS, 3, 256], U8, align_bytes=64)
        i_codes = keep.tile([P, GROUPS, 3, 256], U32, align_bytes=64)
        i_scales = keep.tile([P, GROUPS, 3, 256], U8, align_bytes=64)

        hidden_rows = equivariant_hidden.rearrange("(p s) j c -> p (s j) c", s=8)
        input_rows = invariant_input.rearrange("(p s) c -> p s c", s=8)
        state_rows = invariant_hidden.rearrange("(p s) c -> p s c", s=8)
        out_rows = out.rearrange("(p s) h -> p s h", s=8)
        w_hbm = (W_right, W_left, W_ii[0:512, :], W_ii[512:1024, :], W_ii[1024:1536, :])

        eq_sb, inv_sb, w_raw = {}, {}, {}
        banks, squares, recip, x_grouped, i_grouped, terms, turned, rights = {}, {}, {}, {}, {}, {}, {}, {}

        def load_heads(g):
            with nc.allow_non_contiguous_dma(reason="the first 16 channels arrive in short runs"):
                nc.sync.dma_start(
                    out=head_hidden[:, 6 * g : 6 * g + 6, 0:15], in_=hidden_rows[:, 6 * g : 6 * g + 6, 0:15]
                )

        def load_eq(g, pieces=1):
            eq = acts.tile([P, 6, 512], BF16, tag="eq", align_bytes=64)
            n = 6 // pieces
            for i in range(0, 6, n):
                nc.sync.dma_start(out=eq[:, i : i + n, 16:512], in_=hidden_rows[:, 6 * g + i : 6 * g + i + n, 15:511])
            eq_sb[g] = eq

        def heads(g):
            engine = nc.vector if g == 0 else nc.gpsimd
            engine.tensor_copy(out=eq_sb[g][:, :, 1:16], in_=head_hidden[:, 6 * g : 6 * g + 6, 0:15])
            engine.tensor_copy(out=eq_sb[g][:, :, 0:1], in_=head_input[:, 6 * g : 6 * g + 6].unsqueeze(2))

        def load_inv(pair):
            first = acts.tile([P, 4, 512], BF16, tag="inv_input", bufs=2, align_bytes=64)
            nc.sync.dma_start(out=first[:], in_=input_rows[:, 4 * pair : 4 * pair + 4, :])
            rest = acts.tile([P, 4, 1024], BF16, tag="inv_state", bufs=2, align_bytes=64)
            nc.sync.dma_start(out=rest[:], in_=state_rows[:, 4 * pair : 4 * pair + 4, :])
            inv_sb[pair] = (first, rest)

        def load_w(w):
            raw = stage.tile([P, 4, 1024], BF16, tag="raw", bufs=5)
            nc.sync.dma_start(out=raw[:], in_=w_hbm[w].rearrange("(p t) c -> p t c", t=4))
            w_raw[w] = raw

        def flat(ap):
            return ap.rearrange("p a b -> p (a b)")

        def prepare_w(ws, half):
            n = len(ws)
            grouped = stage.tile([P, n, 512, 4], BF16, tag="grouped%d" % n, bufs=1, align_bytes=64)
            for i, w in enumerate(ws):
                nc.vector.tensor_copy(
                    out=grouped[:, i, :, :].rearrange("p (c i) t -> p c t i", i=4),
                    in_=w_raw[w][:, :, 512 * half : 512 * half + 512].rearrange("p t (c i) -> p c t i", i=4),
                )
            nc.vector.quantize_mx(
                out=flat(w_codes[:, half, ws[0] : ws[0] + n, :]).bitcast(FP8X4),
                scales=flat(w_scales[:, half, ws[0] : ws[0] + n, :]),
                in_=grouped[:].rearrange("p n c t -> p (n c t)"),
            )

        def by_word(ap):
            return ap.rearrange("p (b u e) -> p b u e", u=2, e=2)

        def square(engine, g, s, rows=((0, 3),)):
            sq_tile = work.tile([P, 3, 4, P], F32, tag="square")
            squares[(g, s)] = sq_tile
            for lo, hi in rows:
                src = eq_sb[g][:, 3 * s + lo : 3 * s + hi, :].rearrange("p r (k t) -> p r t k", t=4)
                dst = sq_tile[:, lo:hi, :, :]
                if engine is nc.scalar:
                    nc.scalar.activation(out=dst, in_=src, func=ACT.Square)
                else:
                    nc.vector.tensor_tensor(out=dst, in0=src, in1=src, op=ALU.mult)

        def norm_bank(g, s):
            bank = ring.tile([P, 4, P], F32, tag="ring")
            for t in range(4):
                for j in range(3):
                    nc.tensor.matmul(
                        out=bank[:, t, :],
                        lhsT=squares[(g, s)][:, j, t, :],
                        rhs=ident[:],
                        is_transpose=True,
                        start=(j == 0),
                        stop=(j == 2),
                    )
            banks[("norm", g, s)] = bank[:].rearrange("p t b -> p b t")

        def reciprocal(g, s):
            if g not in recip:
                r_tile = work.tile([P, 2, 512], F32, tag="recip")
                recip[g] = r_tile
            root = work.tile([P, 512], F32, tag="root")
            nc.scalar.activation(
                out=root[:].rearrange("p (b t) -> p b t", t=4),
                in_=banks[("norm", g, s)],
                func=ACT.Abs_reciprocal_sqrt,
                bias=eps[:],
            )
            nc.scalar.activation(out=recip[g][:, s, :], in_=root[:], func=ACT.Square)

        def squares_of(g):
            for s in range(2):
                square(nc.scalar, g, s, rows=((0, 1), (1, 2), (2, 3)))

        def norm(g):
            for s in range(2):
                norm_bank(g, s)
            for s in range(2):
                reciprocal(g, s)

        def eq_bank(g, j):
            words = eq_sb[g][:].bitcast(F32)
            bank = ring.tile([P, 2, 2, P], F32, tag="ring")
            for u in range(2):
                for s in range(2):
                    nc.tensor.transpose(bank[:, u, s, :], words[:, 3 * s + j, u::2], ident[:])
            banks[("eq", g, j)] = bank[:].bitcast(BF16).rearrange("p u s (b e) -> p (s b) u e", e=2)

        def scale_eq(g, j, slots=(0, 2)):
            if g not in x_grouped:
                xg = work.tile([P, 3, 1024], BF16, tag="x_grouped", bufs=1, align_bytes=64)
                x_grouped[g] = xg
            lo, hi = slots
            nc.vector.tensor_tensor(
                out=by_word(x_grouped[g][:, j, 512 * lo : 512 * hi]),
                in0=banks[("eq", g, j)][:, 128 * lo : 128 * hi, :, :],
                in1=by_word(recip[g][:, lo:hi, :].rearrange("p s c -> p (s c)")),
                op=ALU.mult,
            )

        def quantise_x(g, lo, hi):
            nc.vector.quantize_mx(
                out=flat(x_codes[:, g, lo:hi, :]).bitcast(FP8X4),
                scales=flat(x_scales[:, g, lo:hi, :]),
                in_=flat(x_grouped[g][:, lo:hi, :]),
            )

        def inv_bank(g, k):
            source = inv_sb[g // 2][min(k, 1)]
            lo = 256 * max(k - 1, 0)
            words = source[:].bitcast(F32)
            bank = ring.tile([P, 2, 2, P], F32, tag="ring")
            for u in range(2):
                for s in range(2):
                    nc.tensor.transpose(bank[:, u, s, :], words[:, 2 * (g % 2) + s, lo + u : lo + 256 : 2], ident[:])
            banks[("inv", g, k)] = bank[:].rearrange("p u s b -> p (s b) u")

        def copy_inv(g, k):
            if g not in i_grouped:
                ig = work.tile([P, 3, 1024], BF16, tag="i_grouped", bufs=1, align_bytes=64)
                i_grouped[g] = ig
            nc.scalar.copy(out=i_grouped[g][:, k, :].bitcast(F32).rearrange("p (b u) -> p b u", u=2), in_=banks[("inv", g, k)])

        def quantise_inv(g, lo, hi):
            nc.vector.quantize_mx(
                out=flat(i_codes[:, g, lo:hi, :]).bitcast(FP8X4),
                scales=flat(i_scales[:, g, lo:hi, :]),
                in_=flat(i_grouped[g][:, lo:hi, :]),
            )

        def mx(acc, w, h_tile, codes, scales, row, g, start, stop):
            half, tile_of_half = divmod(h_tile, 4)
            h_cols = slice(128 * tile_of_half, 128 * tile_of_half + 128)
            nc.tensor.matmul_mx(
                out=acc,
                lhsT=w_codes[:, half, w, h_cols].bitcast(FP8X4),
                lhsT_scale=w_scales[:, half, w, h_cols],
                rhs=codes[:, g, row, :].bitcast(FP8X4),
                rhs_scale=scales[:, g, row, :],
                start=start,
                stop=stop,
            )

        def right_product(r, j):
            g, quarter = ORDER[r]
            right = ring.tile([P, 2, 256], F32, tag="ring")
            for i in range(2):
                mx(right[:, i, :], W_R, 2 * quarter + i, x_codes, x_scales, j, g, True, True)
            right_sb = block.tile([P, 2, 256], F32, tag="right", bufs=6)
            nc.scalar.copy(out=right_sb[:], in_=right[:])
            rights[(r, j)] = right_sb

        def left_product(r, j):
            g, quarter = ORDER[r]
            left = ring.tile([P, 2, 256], F32, tag="ring")
            for i in range(2):
                mx(left[:, i, :], W_L, 2 * quarter + i, x_codes, x_scales, j, g, True, True)
            term = block.tile([P, 2, 256], F32, tag="term%d" % j, bufs=5)
            nc.vector.tensor_tensor(out=term[:], in0=left[:], in1=rights[(r, j)][:], op=ALU.mult)
            terms[(r, j)] = term

        def linear(r):
            g, quarter = ORDER[r]
            lin = ring.tile([P, 2, 256], F32, tag="ring")
            for i in range(2):
                for k in range(3):
                    mx(lin[:, i, :], W_I + k, 2 * quarter + i, i_codes, i_scales, k, g, k == 0, k == 2)
            for i in range(2):
                nc.vector.scalar_tensor_tensor(
                    out=terms[(r, 0)][:, i, :],
                    in0=lin[:, i, :],
                    scalar=bias[:, 2 * quarter + i : 2 * quarter + i + 1],
                    in1=terms[(r, 0)][:, i, :],
                    op0=ALU.add,
                    op1=ALU.add,
                )

        def tensor_adds(r):
            return r < 1 or r >= ROUNDS - 2

        def add_terms(r, j):
            if not tensor_adds(r):
                for i in range(2):
                    total, term = terms[(r, j - 1)][:, i, :], terms[(r, j)][:, i, :]
                    nc.gpsimd.tensor_tensor(out=total, in0=total, in1=term, op=ALU.add)

        def slot_runs(r):
            return ((0, 2),) if r < ROUNDS - 1 else ((0, 1), (1, 2))

        def turn_back(r):
            n_terms = 3 if tensor_adds(r) else 1
            for lo, hi in slot_runs(r):
                bank = ring.tile([P, hi - lo, 2, P], F32, tag="ring")
                for s in range(lo, hi):
                    for i in range(2):
                        for j in range(n_terms):
                            nc.tensor.matmul(
                                out=bank[:, s - lo, i, :],
                                lhsT=terms[(r, j)][:, i, 128 * s : 128 * s + 128],
                                rhs=ident[:],
                                is_transpose=True,
                                start=(j == 0),
                                stop=(j == n_terms - 1),
                            )
                turned[(r, lo)] = bank

        def finish(r):
            g, quarter = ORDER[r]
            for lo, hi in slot_runs(r):
                res = block.tile([P, hi - lo, 256], F32, tag="res", bufs=5)
                nc.scalar.activation(out=res[:], in_=turned[(r, lo)][:].rearrange("p s i h -> p s (i h)"), func=ACT.Tanh)
                nc.sync.dma_start(
                    out=out_rows[:, 2 * g + lo : 2 * g + hi, 256 * quarter : 256 * quarter + 256], in_=res[:]
                )

        with nc.allow_non_contiguous_dma(reason="the first 16 channels arrive in short runs"):
            load_heads(0)
            nc.sync.dma_start(out=head_input[:], in_=equivariant_input.rearrange("(p s) j -> p (s j)", s=8))
            load_eq(0, pieces=2)
        nc.vector.memset(bias_rows[:], 0.0)
        nc.gpsimd.dma_start(out=bias_rows[0:8, :], in_=b_ii.rearrange("(r c) -> r c", c=P))
        load_w(W_R)
        load_w(W_L)
        load_heads(1)
        load_eq(1)
        load_inv(0)
        load_w(W_I)
        load_w(W_I + 1)
        load_w(W_I + 2)
        load_heads(2)
        load_eq(2)
        load_heads(3)
        load_eq(3)
        load_inv(1)

        with tc.manual_schedule():
            heads(0)
            square(nc.scalar, 0, 0)
            square(nc.vector, 0, 1)
            for s in range(2):
                eq_bank(0, s)
                norm_bank(0, s)
                reciprocal(0, s)
            eq_bank(0, 2)
            prepare_w((W_R,), 0)
            for j in range(3):
                scale_eq(0, j, slots=(0, 1))
            for j in range(2):
                scale_eq(0, j, slots=(1, 2))
            quantise_x(0, 0, 1)
            scale_eq(0, 2, slots=(1, 2))
            heads(1)
            quantise_x(0, 1, 3)
            prepare_w((W_L,), 0)
            squares_of(1)
        INV_ROUND = {0: 0, 1: 1, 7: 2, 10: 3}
        X_ROUND = {3: ((2, 0),), 5: ((2, 1),), 6: ((2, 2),), 7: ((3, 0),), 9: ((3, 1), (3, 2))}

        def banks_for(r):
            if r in INV_ROUND:
                for k in range(2):
                    inv_bank(INV_ROUND[r], k)
            for g, j in X_ROUND.get(r, ()):
                eq_bank(g, j)

        def before_products(r):
            for g, j in X_ROUND.get(r - 1, ()):
                if j > 0:
                    quantise_x(g, 2 * j - 2, j + 1)

        def behind_products(r):
            if r - 1 in INV_ROUND:
                quantise_inv(INV_ROUND[r - 1], 0, 2)
                quantise_inv(INV_ROUND[r - 1], 2, 3)
            for g, j in X_ROUND.get(r, ()):
                scale_eq(g, j)

        def side_work(r):
            if r == 0:
                norm(1)
                for j in range(3):
                    eq_bank(1, j)
                for j in range(3):
                    scale_eq(1, j)
                quantise_x(1, 0, 2)
                quantise_x(1, 2, 3)
            if r in (0, 2):
                heads(2 + r // 2)
                squares_of(2 + r // 2)
            if r == 0:
                banks_for(0)
            if r in INV_ROUND:
                for k in range(3):
                    if k == 2:
                        inv_bank(INV_ROUND[r], k)
                    copy_inv(INV_ROUND[r], k)
            if r == 1:
                bias_ps = ring.tile([P, P], BF16, tag="ring")
                nc.tensor.transpose(bias_ps[:], bias_rows[:], ident_bf[:])
                nc.vector.tensor_copy(out=bias[:], in_=bias_ps[:, 0:8])
                prepare_w((W_I, W_I + 1), 0)
                prepare_w((W_I + 2,), 0)
                prepare_w((W_R, W_L), 1)
            if r == 2:
                for g in (2, 3):
                    norm(g)
                prepare_w((W_I, W_I + 1), 1)
            if r == 4:
                prepare_w((W_I + 2,), 1)

        def lin_round(v):
            return v + (2 if v < 6 else 1 if v < 14 else 0)

        def turn_round(v):
            return lin_round(v) + 1

        def linear_parts(r):
            for v in range(ROUNDS):
                if lin_round(v) == r:
                    linear(v)
                    add_terms(v, 1)

        for j in range(3):
            right_product(0, j)
        for r in range(ROUNDS + 1):
            before_products(r)
            for j in range(3):
                if r + 1 < ROUNDS:
                    right_product(r + 1, j)
                if r < ROUNDS:
                    left_product(r, j)
                if j == (1 if r < ROUNDS - 1 else 0):
                    linear_parts(r)
                if j == 1:
                    behind_products(r)
            if r < ROUNDS:
                add_terms(r, 2)
            side_work(r)
            banks_for(r + 1)
            for v in range(ROUNDS):
                if turn_round(v) == r:
                    turn_back(v)
            for v in range(ROUNDS):
                if turn_round(v) == r:
                    finish(v)
